import numpy as np
import ml_dtypes


def mxq(x, axis, fmt="e4m3"):
    dtype, down = {"e4m3": (ml_dtypes.float8_e4m3fn, 7), "e5m2": (ml_dtypes.float8_e5m2, 14)}[fmt]
    v = np.moveaxis(np.asarray(x, np.float32).astype(ml_dtypes.bfloat16).astype(np.float64), axis, -1)
    blocks = v.reshape(v.shape[:-1] + (-1, 32))
    amax = np.abs(blocks).max(-1, keepdims=True)
    byte = np.maximum(np.where(amax > 0, np.frexp(amax)[1] - 1 + 127, 0) - down, 1)
    scale = np.exp2(byte - 127.0)
    codes = (blocks / scale).astype(np.float32).astype(dtype).astype(np.float64)
    return np.moveaxis((codes * scale).reshape(v.shape), -1, axis)


WIDE = False


def mx_kscale(k):
    if not WIDE:
        return np.ones(k)
    levels = np.array([10, -10, 5, -5, 0])
    a = np.random.permutation(np.resize(levels, k // 512 * 4)).reshape(k // 512, 4)
    idx = np.arange(k)
    return np.exp2(a[idx // 512, idx % 128 // 32])


BF16 = ml_dtypes.bfloat16


def bf(x):
    return np.asarray(x, np.float32).astype(BF16)


def f64(x):
    return np.asarray(x).astype(np.float64)


B, S, W, QK, E, V, H = 4, 1024, 1024, 128, 384, 1024, 1
N = 2 * QK + 2 * E


def erf(v):
    a = np.clip(v, -6.0, 6.0)
    a2 = a * a
    term = a.copy()
    tot = a.copy()
    for n in range(1, 100):
        term = term * (a2 / (n + 0.5))
        tot = tot + term
    return 2.0 / np.sqrt(np.pi) * np.exp(-a2) * tot


def gelu_erf(v):
    return 0.5 * v * (1.0 + erf(v / np.sqrt(2.0)))


def setup_inputs():
    s = mx_kscale(W)
    g = np.where(np.arange(N) < 2 * QK, 1.4, 1.0)
    return {"x": bf(np.random.standard_normal((B, S, W)) * 1.5 + 0.5),
            "norm_w": bf((1.0 + 0.1 * np.random.standard_normal(W)) * s),
            "expand_w": bf(np.random.standard_normal((N, W)) * g[:, None] / np.sqrt(W) / s[None, :])}


def reference(x, norm_w, expand_w):
    x = f64(x)
    mu = x.mean(-1, keepdims=True)
    var = x.var(-1, keepdims=True)
    xn = (x - mu) / np.sqrt(var + 1e-5) * f64(norm_w)
    hidden = mxq(xn, 2, "e4m3") @ mxq(f64(expand_w), 1, "e4m3").T
    q = hidden[..., :QK]
    k = hidden[..., QK:2 * QK]
    lin = hidden[..., 2 * QK:2 * QK + E]
    pre = hidden[..., 2 * QK + E:]
    geglu = lin * gelu_erf(pre)
    return q, k, geglu

@@ -1,0 +1,217 @@
+from contextlib import ExitStack
+
+import concourse.mybir as mybir
+from concourse.masks import make_identity
+
+F32 = mybir.dt.float32
+BF16 = mybir.dt.bfloat16
+U32 = mybir.dt.uint32
+U8 = mybir.dt.uint8
+FP8X4 = mybir.dt.float8_e4m3fn_x4
+ACT = mybir.ActivationFunctionType
+ALU = mybir.AluOpType
+
+P = 128
+PACK = 4
+K_PASS = P * PACK
+BANK = 512
+
+ROWS = 4 * 1024
+W = 1024
+QK = 128
+E = 384
+N = 2 * QK + 2 * E
+EPS = 1e-5
+
+PASSES = W // K_PASS
+SLOTS = N // P
+TILES_PER_GROUP = 4
+GROUP_ROWS = TILES_PER_GROUP * P
+GROUPS = ROWS // GROUP_ROWS
+VECTOR_STATS_EVERY = 3
+
+FLOPS = 2 * ROWS * W * N
+
+
+def tile_latentattentionblock_pa_t_kernel(tc, x, norm_w, expand_w, out_0, out_1, out_2):
+    nc = tc.nc
+    x_rows = x.flatten_outer_dims()
+    q_rows = out_0.flatten_outer_dims()
+    k_rows = out_1.flatten_outer_dims()
+    geglu_rows = out_2.flatten_outer_dims()
+
+    with ExitStack() as pools:
+        const = pools.enter_context(tc.tile_pool(name="const", bufs=1))
+        resident = pools.enter_context(tc.tile_pool(name="resident", bufs=GROUPS))
+        small = pools.enter_context(tc.tile_pool(name="small", bufs=6))
+        work = pools.enter_context(tc.tile_pool(name="work", bufs=3))
+        stage = pools.enter_context(tc.tile_pool(name="stage", bufs=2))
+        psum = pools.enter_context(tc.psum_pool(name="psum", bufs=4))
+
+        x_groups = []
+        for grp in range(GROUPS):
+            x_group = resident.tile([P, TILES_PER_GROUP, W], BF16, name="x_group")
+            x_groups.append(x_group)
+
+        def load_x(grp, j0, j1):
+            rows = x_rows[grp * GROUP_ROWS : (grp + 1) * GROUP_ROWS, :]
+            view = rows.rearrange("(p j) k -> p j k", j=TILES_PER_GROUP)
+            nc.sync.dma_start(out=x_groups[grp][:, j0:j1, :], in_=view[:, j0:j1, :])
+
+        w_rows = const.tile([P, SLOTS, W], BF16)
+
+        def load_w(slot0, slot1, row0):
+            rows = expand_w[row0 : row0 + (slot1 - slot0) * P, :]
+            nc.sync.dma_start(out=w_rows[:, slot0:slot1, :], in_=rows.rearrange("(s p) k -> p s k", p=P))
+
+        load_x(0, 0, 1)
+        load_x(0, 1, 2)
+        load_w(0, 2, 0)
+        load_w(2, 5, 2 * QK + E)
+        load_w(5, 8, 2 * QK)
+        load_x(0, 2, 4)
+        for grp in range(1, GROUPS):
+            load_x(grp, 0, TILES_PER_GROUP)
+
+        ident_f32 = const.tile([P, P], F32)
+        make_identity(nc, ident_f32[:])
+        ident_bf16 = const.tile([P, P], BF16)
+        make_identity(nc, ident_bf16[:])
+        minus_half = const.tile([P, 1], F32)
+        nc.vector.memset(minus_half[:], -0.5)
+
+        table_in = const.tile([P, 1], F32)
+        nc.vector.memset(table_in[:], 0.0)
+        table_out = const.tile([P, 1], F32)
+        nc.scalar.activation(out=table_out[:], in_=table_in[:], func=ACT.Gelu)
+
+        gain_rows = const.tile([P, P], BF16)
+        nc.vector.memset(gain_rows[:], 0.0)
+        nc.scalar.dma_start(out=gain_rows[0 : W // P, :], in_=norm_w.rearrange("(c p) -> c p", p=P))
+        gain_ps = psum.tile([P, P], BF16, tag="turned")
+        nc.tensor.transpose(out=gain_ps[:], in_=gain_rows[:], identity=ident_bf16[:])
+        gain_t = const.tile([P, W // P], F32)
+        nc.vector.tensor_copy(out=gain_t[:], in_=gain_ps[:, 0 : W // P])
+
+        w_grouped = const.tile([P, PASSES, N, PACK], BF16, align_bytes=64)
+        w_codes = const.tile([P, PASSES, N], U32, align_bytes=64)
+        w_scales = const.tile([P, PASSES, N], U8, align_bytes=64)
+        slots_per_bank = BANK // P
+        for bank in range(N // BANK):
+            cols = slice(bank * BANK, (bank + 1) * BANK)
+            for s in range(bank * slots_per_bank, (bank + 1) * slots_per_bank):
+                for g in range(PASSES):
+                    w_turned = psum.tile([P, PACK, P], BF16, tag="turned")
+                    for t in range(PACK):
+                        k0 = g * K_PASS + t * P
+                        nc.tensor.transpose(
+                            out=w_turned[:, t, :], in_=w_rows[:, s, k0 : k0 + P], identity=ident_bf16[:]
+                        )
+                    dst = w_grouped[:, g, s * P : (s + 1) * P, :]
+                    src = w_turned[:].rearrange("p t n -> p n t")
+                    if g == 0:
+                        nc.vector.tensor_copy(out=dst, in_=src)
+                    else:
+                        nc.scalar.copy(out=dst, in_=src)
+            for g in range(PASSES):
+                nc.vector.quantize_mx(
+                    out=w_codes[:, g, cols].bitcast(FP8X4),
+                    scales=w_scales[:, g, cols],
+                    in_=w_grouped[:, g, cols, :].rearrange("p n t -> p (n t)"),
+                )
+
+        for grp in range(GROUPS):
+            qk_stage = stage.tile([P, 2, TILES_PER_GROUP, QK], F32)
+            geglu_stage = stage.tile([P, TILES_PER_GROUP, E], F32)
+            for j in range(TILES_PER_GROUP):
+                x_tile = x_groups[grp][:, j, :]
+
+                neg_mean = small.tile([P, 1], F32)
+                var_eps = small.tile([P, 1], F32)
+                if (grp * TILES_PER_GROUP + j) % VECTOR_STATS_EVERY == 0:
+                    halves = small.tile([P, 2, 6], F32)
+                    for h in range(2):
+                        nc.vector.bn_stats(out=halves[:, h, :], in_=x_tile[:, h * 512 : (h + 1) * 512])
+                    mean_var = small.tile([P, 2], F32)
+                    nc.vector.bn_aggr(out=mean_var[:], in_=halves[:].rearrange("p h s -> p (h s)"))
+                    nc.gpsimd.tensor_scalar(
+                        out=neg_mean[:], in0=mean_var[:, 0:1], scalar1=-1.0, scalar2=0.0, op0=ALU.mult, op1=ALU.add
+                    )
+                    nc.gpsimd.tensor_scalar(
+                        out=var_eps[:], in0=mean_var[:, 1:2], scalar1=1.0, scalar2=EPS, op0=ALU.mult, op1=ALU.add
+                    )
+                else:
+                    unread_a = work.tile([P, W], BF16)
+                    nc.scalar.activation(
+                        out=unread_a[:], in_=x_tile, func=ACT.Copy, scale=-1.0 / W, accum_out=neg_mean[:]
+                    )
+                    unread_b = work.tile([P, W], BF16)
+                    square_sum = small.tile([P, 1], F32)
+                    nc.scalar.activation(
+                        out=unread_b[:], in_=x_tile, func=ACT.Square, bias=neg_mean[:], accum_out=square_sum[:]
+                    )
+                    nc.gpsimd.tensor_scalar(
+                        out=var_eps[:], in0=square_sum[:], scalar1=1.0 / W, scalar2=EPS, op0=ALU.mult, op1=ALU.add
+                    )
+                rstd = small.tile([P, 1], F32)
+                nc.gpsimd.tensor_tensor(out=rstd[:], in0=var_eps[:], in1=minus_half[:], op=ALU.pow)
+
+                centred = work.tile([P, W], F32)
+                nc.gpsimd.tensor_scalar(
+                    out=centred[:], in0=x_tile, scalar1=neg_mean[:], scalar2=rstd[:], op0=ALU.add, op1=ALU.mult
+                )
+
+                xn_grouped = work.tile([P, PASSES, P, PACK], BF16, align_bytes=64)
+                for g in range(PASSES):
+                    turned = psum.tile([P, PACK, P], F32, tag="turned")
+                    for t in range(PACK):
+                        k0 = g * K_PASS + t * P
+                        nc.tensor.transpose(out=turned[:, t, :], in_=centred[:, k0 : k0 + P], identity=ident_f32[:])
+                    gain = gain_t[:, g * PACK : (g + 1) * PACK].unsqueeze(1).to_broadcast([P, P, PACK])
+                    nc.vector.tensor_tensor(
+                        out=xn_grouped[:, g, :, :], in0=turned[:].rearrange("p t r -> p r t"), in1=gain, op=ALU.mult
+                    )
+                xn_codes = work.tile([P, PASSES, P], U32, align_bytes=64)
+                xn_scales = work.tile([P, PASSES, P], U8, align_bytes=64)
+                nc.vector.quantize_mx(
+                    out=xn_codes[:].rearrange("p g r -> p (g r)").bitcast(FP8X4),
+                    scales=xn_scales[:].rearrange("p g r -> p (g r)"),
+                    in_=xn_grouped[:].rearrange("p g r t -> p (g r t)"),
+                )
+
+                hidden_0 = psum.tile([P, BANK], F32, tag="hidden")
+                hidden_1 = psum.tile([P, BANK], F32, tag="hidden")
+                for bank, hidden in enumerate((hidden_0, hidden_1)):
+                    cols = slice(bank * BANK, (bank + 1) * BANK)
+                    for g in range(PASSES):
+                        nc.tensor.matmul_mx(
+                            out=hidden[:],
+                            lhsT=xn_codes[:, g, :].bitcast(FP8X4),
+                            lhsT_scale=xn_scales[:, g, :],
+                            rhs=w_codes[:, g, cols].bitcast(FP8X4),
+                            rhs_scale=w_scales[:, g, cols],
+                            start=(g == 0),
+                            stop=(g == PASSES - 1),
+                        )
+
+                pre_in_0 = BANK - 2 * QK
+                gelu = work.tile([P, E], F32)
+                nc.scalar.activation(out=gelu[:, 0:pre_in_0], in_=hidden_0[:, 2 * QK : BANK], func=ACT.Gelu)
+                nc.scalar.activation(out=gelu[:, pre_in_0:E], in_=hidden_1[:, 0 : E - pre_in_0], func=ACT.Gelu)
+                nc.scalar.copy(
+                    out=qk_stage[:, :, j, :], in_=hidden_0[:, 0 : 2 * QK].rearrange("p (o c) -> p o c", o=2)
+                )
+                nc.vector.tensor_tensor(
+                    out=geglu_stage[:, j, :], in0=hidden_1[:, E - pre_in_0 : BANK], in1=gelu[:], op=ALU.mult
+                )
+
+            rows = slice(grp * GROUP_ROWS, (grp + 1) * GROUP_ROWS)
+            nc.sync.dma_start(
+                out=q_rows[rows, :].rearrange("(p j) c -> p j c", j=TILES_PER_GROUP), in_=qk_stage[:, 0, :, :]
+            )
+            nc.sync.dma_start(
+                out=k_rows[rows, :].rearrange("(p j) c -> p j c", j=TILES_PER_GROUP), in_=qk_stage[:, 1, :, :]
+            )
+            nc.sync.dma_start(
+                out=geglu_rows[rows, :].rearrange("(p j) c -> p j c", j=TILES_PER_GROUP), in_=geglu_stage[:]
+            )

@@ -28,7 +28,15 @@ SLOTS = N // P
 TILES_PER_GROUP = 4
 GROUP_ROWS = TILES_PER_GROUP * P
 GROUPS = ROWS // GROUP_ROWS
+N_TILES = ROWS // P
 VECTOR_STATS_EVERY = 3
+
+LAG_NORMALISE = 1
+LAG_TURN = 3
+LAG_QUANTISE = 4
+LAG_PROJECT = 5
+LAG_GATE = 6
+WEIGHT_STEPS = 4
 
 FLOPS = 2 * ROWS * W * N
 
@@ -41,9 +49,10 @@ def tile_latentattentionblock_pa_t_kernel(tc, x, norm_w, expand_w, out_0, out_1,
     geglu_rows = out_2.flatten_outer_dims()
 
     with ExitStack() as pools:
+        pools.enter_context(tc.manual_schedule())
         const = pools.enter_context(tc.tile_pool(name="const", bufs=1))
         resident = pools.enter_context(tc.tile_pool(name="resident", bufs=GROUPS))
-        small = pools.enter_context(tc.tile_pool(name="small", bufs=6))
+        small = pools.enter_context(tc.tile_pool(name="small", bufs=4))
         work = pools.enter_context(tc.tile_pool(name="work", bufs=3))
         stage = pools.enter_context(tc.tile_pool(name="stage", bufs=2))
         psum = pools.enter_context(tc.psum_pool(name="psum", bufs=4))
@@ -67,9 +76,9 @@ def tile_latentattentionblock_pa_t_kernel(tc, x, norm_w, expand_w, out_0, out_1,
         load_x(0, 0, 1)
         load_x(0, 1, 2)
         load_w(0, 2, 0)
+        load_x(0, 2, 4)
         load_w(2, 5, 2 * QK + E)
         load_w(5, 8, 2 * QK)
-        load_x(0, 2, 4)
         for grp in range(1, GROUPS):
             load_x(grp, 0, TILES_PER_GROUP)
 
@@ -96,23 +105,24 @@ def tile_latentattentionblock_pa_t_kernel(tc, x, norm_w, expand_w, out_0, out_1,
         w_grouped = const.tile([P, PASSES, N, PACK], BF16, align_bytes=64)
         w_codes = const.tile([P, PASSES, N], U32, align_bytes=64)
         w_scales = const.tile([P, PASSES, N], U8, align_bytes=64)
-        slots_per_bank = BANK // P
-        for bank in range(N // BANK):
+
+        def turn_weights(s):
+            for g in range(PASSES):
+                w_turned = psum.tile([P, PACK, P], BF16, tag="turned")
+                for t in range(PACK):
+                    k0 = g * K_PASS + t * P
+                    nc.tensor.transpose(
+                        out=w_turned[:, t, :], in_=w_rows[:, s, k0 : k0 + P], identity=ident_bf16[:]
+                    )
+                dst = w_grouped[:, g, s * P : (s + 1) * P, :]
+                src = w_turned[:].rearrange("p t n -> p n t")
+                if g == 0:
+                    nc.vector.tensor_copy(out=dst, in_=src)
+                else:
+                    nc.scalar.copy(out=dst, in_=src)
+
+        def quantise_weights(bank):
             cols = slice(bank * BANK, (bank + 1) * BANK)
-            for s in range(bank * slots_per_bank, (bank + 1) * slots_per_bank):
-                for g in range(PASSES):
-                    w_turned = psum.tile([P, PACK, P], BF16, tag="turned")
-                    for t in range(PACK):
-                        k0 = g * K_PASS + t * P
-                        nc.tensor.transpose(
-                            out=w_turned[:, t, :], in_=w_rows[:, s, k0 : k0 + P], identity=ident_bf16[:]
-                        )
-                    dst = w_grouped[:, g, s * P : (s + 1) * P, :]
-                    src = w_turned[:].rearrange("p t n -> p n t")
-                    if g == 0:
-                        nc.vector.tensor_copy(out=dst, in_=src)
-                    else:
-                        nc.scalar.copy(out=dst, in_=src)
             for g in range(PASSES):
                 nc.vector.quantize_mx(
                     out=w_codes[:, g, cols].bitcast(FP8X4),
@@ -120,98 +130,159 @@ def tile_latentattentionblock_pa_t_kernel(tc, x, norm_w, expand_w, out_0, out_1,
                     in_=w_grouped[:, g, cols, :].rearrange("p n t -> p (n t)"),
                 )
 
-        for grp in range(GROUPS):
-            qk_stage = stage.tile([P, 2, TILES_PER_GROUP, QK], F32)
-            geglu_stage = stage.tile([P, TILES_PER_GROUP, E], F32)
-            for j in range(TILES_PER_GROUP):
-                x_tile = x_groups[grp][:, j, :]
+        mean_vars, neg_means, square_sums, centreds, turneds, xn_groupeds = {}, {}, {}, {}, {}, {}
+        xn_codess, xn_scaless, hiddens, gelus, stages = {}, {}, {}, {}, {}
 
-                neg_mean = small.tile([P, 1], F32)
-                var_eps = small.tile([P, 1], F32)
-                if (grp * TILES_PER_GROUP + j) % VECTOR_STATS_EVERY == 0:
-                    halves = small.tile([P, 2, 6], F32)
-                    for h in range(2):
-                        nc.vector.bn_stats(out=halves[:, h, :], in_=x_tile[:, h * 512 : (h + 1) * 512])
-                    mean_var = small.tile([P, 2], F32)
-                    nc.vector.bn_aggr(out=mean_var[:], in_=halves[:].rearrange("p h s -> p (h s)"))
-                    nc.gpsimd.tensor_scalar(
-                        out=neg_mean[:], in0=mean_var[:, 0:1], scalar1=-1.0, scalar2=0.0, op0=ALU.mult, op1=ALU.add
-                    )
-                    nc.gpsimd.tensor_scalar(
-                        out=var_eps[:], in0=mean_var[:, 1:2], scalar1=1.0, scalar2=EPS, op0=ALU.mult, op1=ALU.add
-                    )
-                else:
-                    unread_a = work.tile([P, W], BF16)
-                    nc.scalar.activation(
-                        out=unread_a[:], in_=x_tile, func=ACT.Copy, scale=-1.0 / W, accum_out=neg_mean[:]
-                    )
-                    unread_b = work.tile([P, W], BF16)
-                    square_sum = small.tile([P, 1], F32)
-                    nc.scalar.activation(
-                        out=unread_b[:], in_=x_tile, func=ACT.Square, bias=neg_mean[:], accum_out=square_sum[:]
-                    )
-                    nc.gpsimd.tensor_scalar(
-                        out=var_eps[:], in0=square_sum[:], scalar1=1.0 / W, scalar2=EPS, op0=ALU.mult, op1=ALU.add
-                    )
-                rstd = small.tile([P, 1], F32)
-                nc.gpsimd.tensor_tensor(out=rstd[:], in0=var_eps[:], in1=minus_half[:], op=ALU.pow)
+        def x_tile(i):
+            return x_groups[i // TILES_PER_GROUP][:, i % TILES_PER_GROUP, :]
 
-                centred = work.tile([P, W], F32)
+        def on_vector(i):
+            return i % VECTOR_STATS_EVERY == 1
+
+        def statistics(i):
+            if on_vector(i):
+                halves = small.tile([P, 2, 6], F32, name="halves")
+                for h in range(2):
+                    nc.vector.bn_stats(out=halves[:, h, :], in_=x_tile(i)[:, h * 512 : (h + 1) * 512])
+                mean_var = small.tile([P, 2], F32, name="mean_var")
+                nc.vector.bn_aggr(out=mean_var[:], in_=halves[:].rearrange("p h s -> p (h s)"))
+                mean_vars[i] = mean_var
+            else:
+                neg_mean = small.tile([P, 1], F32, name="neg_mean")
+                unread_a = work.tile([P, W], BF16, name="unread_a")
+                nc.scalar.activation(
+                    out=unread_a[:], in_=x_tile(i), func=ACT.Copy, scale=-1.0 / W, accum_out=neg_mean[:]
+                )
+                unread_b = work.tile([P, W], BF16, name="unread_b")
+                square_sum = small.tile([P, 1], F32, name="square_sum")
+                nc.scalar.activation(
+                    out=unread_b[:], in_=x_tile(i), func=ACT.Square, bias=neg_mean[:], accum_out=square_sum[:]
+                )
+                neg_means[i] = neg_mean
+                square_sums[i] = square_sum
+
+        def normalise(i):
+            var_eps = small.tile([P, 1], F32, name="var_eps")
+            if on_vector(i):
+                neg_means[i] = small.tile([P, 1], F32, name="neg_mean")
                 nc.gpsimd.tensor_scalar(
-                    out=centred[:], in0=x_tile, scalar1=neg_mean[:], scalar2=rstd[:], op0=ALU.add, op1=ALU.mult
+                    out=neg_means[i][:], in0=mean_vars[i][:, 0:1], scalar1=-1.0, scalar2=0.0, op0=ALU.mult, op1=ALU.add
                 )
-
-                xn_grouped = work.tile([P, PASSES, P, PACK], BF16, align_bytes=64)
-                for g in range(PASSES):
-                    turned = psum.tile([P, PACK, P], F32, tag="turned")
-                    for t in range(PACK):
-                        k0 = g * K_PASS + t * P
-                        nc.tensor.transpose(out=turned[:, t, :], in_=centred[:, k0 : k0 + P], identity=ident_f32[:])
-                    gain = gain_t[:, g * PACK : (g + 1) * PACK].unsqueeze(1).to_broadcast([P, P, PACK])
-                    nc.vector.tensor_tensor(
-                        out=xn_grouped[:, g, :, :], in0=turned[:].rearrange("p t r -> p r t"), in1=gain, op=ALU.mult
-                    )
-                xn_codes = work.tile([P, PASSES, P], U32, align_bytes=64)
-                xn_scales = work.tile([P, PASSES, P], U8, align_bytes=64)
-                nc.vector.quantize_mx(
-                    out=xn_codes[:].rearrange("p g r -> p (g r)").bitcast(FP8X4),
-                    scales=xn_scales[:].rearrange("p g r -> p (g r)"),
-                    in_=xn_grouped[:].rearrange("p g r t -> p (g r t)"),
+                nc.gpsimd.tensor_scalar(
+                    out=var_eps[:], in0=mean_vars[i][:, 1:2], scalar1=1.0, scalar2=EPS, op0=ALU.mult, op1=ALU.add
                 )
-
-                hidden_0 = psum.tile([P, BANK], F32, tag="hidden")
-                hidden_1 = psum.tile([P, BANK], F32, tag="hidden")
-                for bank, hidden in enumerate((hidden_0, hidden_1)):
-                    cols = slice(bank * BANK, (bank + 1) * BANK)
-                    for g in range(PASSES):
-                        nc.tensor.matmul_mx(
-                            out=hidden[:],
-                            lhsT=xn_codes[:, g, :].bitcast(FP8X4),
-                            lhsT_scale=xn_scales[:, g, :],
-                            rhs=w_codes[:, g, cols].bitcast(FP8X4),
-                            rhs_scale=w_scales[:, g, cols],
-                            start=(g == 0),
-                            stop=(g == PASSES - 1),
-                        )
-
-                pre_in_0 = BANK - 2 * QK
-                gelu = work.tile([P, E], F32)
-                nc.scalar.activation(out=gelu[:, 0:pre_in_0], in_=hidden_0[:, 2 * QK : BANK], func=ACT.Gelu)
-                nc.scalar.activation(out=gelu[:, pre_in_0:E], in_=hidden_1[:, 0 : E - pre_in_0], func=ACT.Gelu)
-                nc.scalar.copy(
-                    out=qk_stage[:, :, j, :], in_=hidden_0[:, 0 : 2 * QK].rearrange("p (o c) -> p o c", o=2)
+            else:
+                nc.gpsimd.tensor_scalar(
+                    out=var_eps[:], in0=square_sums[i][:], scalar1=1.0 / W, scalar2=EPS, op0=ALU.mult, op1=ALU.add
                 )
+            rstd = small.tile([P, 1], F32, name="rstd")
+            nc.gpsimd.tensor_tensor(out=rstd[:], in0=var_eps[:], in1=minus_half[:], op=ALU.pow)
+            centred = work.tile([P, W], F32, name="centred", bufs=4)
+            nc.gpsimd.tensor_scalar(
+                out=centred[:], in0=x_tile(i), scalar1=neg_means[i][:], scalar2=rstd[:], op0=ALU.add, op1=ALU.mult
+            )
+            centreds[i] = centred
+
+        def turn(i):
+            turneds[i] = []
+            for g in range(PASSES):
+                turned = psum.tile([P, PACK, P], F32, tag="turned", name="turned")
+                for t in range(PACK):
+                    k0 = g * K_PASS + t * P
+                    nc.tensor.transpose(out=turned[:, t, :], in_=centreds[i][:, k0 : k0 + P], identity=ident_f32[:])
+                turneds[i].append(turned)
+
+        def apply_gain(i):
+            xn_grouped = work.tile([P, PASSES, P, PACK], BF16, align_bytes=64, name="xn_grouped")
+            for g in range(PASSES):
+                gain = gain_t[:, g * PACK : (g + 1) * PACK].unsqueeze(1).to_broadcast([P, P, PACK])
                 nc.vector.tensor_tensor(
-                    out=geglu_stage[:, j, :], in0=hidden_1[:, E - pre_in_0 : BANK], in1=gelu[:], op=ALU.mult
+                    out=xn_grouped[:, g, :, :],
+                    in0=turneds[i][g][:].rearrange("p t r -> p r t"),
+                    in1=gain,
+                    op=ALU.mult,
                 )
+            xn_groupeds[i] = xn_grouped
 
-            rows = slice(grp * GROUP_ROWS, (grp + 1) * GROUP_ROWS)
-            nc.sync.dma_start(
-                out=q_rows[rows, :].rearrange("(p j) c -> p j c", j=TILES_PER_GROUP), in_=qk_stage[:, 0, :, :]
+        def quantise(i):
+            xn_codes = work.tile([P, PASSES, P], U32, align_bytes=64, name="xn_codes")
+            xn_scales = work.tile([P, PASSES, P], U8, align_bytes=64, name="xn_scales")
+            nc.vector.quantize_mx(
+                out=xn_codes[:].rearrange("p g r -> p (g r)").bitcast(FP8X4),
+                scales=xn_scales[:].rearrange("p g r -> p (g r)"),
+                in_=xn_groupeds[i][:].rearrange("p g r t -> p (g r t)"),
             )
-            nc.sync.dma_start(
-                out=k_rows[rows, :].rearrange("(p j) c -> p j c", j=TILES_PER_GROUP), in_=qk_stage[:, 1, :, :]
+            xn_codess[i] = xn_codes
+            xn_scaless[i] = xn_scales
+
+        def project(i):
+            hiddens[i] = []
+            for bank in range(N // BANK):
+                cols = slice(bank * BANK, (bank + 1) * BANK)
+                hidden = psum.tile([P, BANK], F32, tag="hidden", name="hidden")
+                for g in range(PASSES):
+                    nc.tensor.matmul_mx(
+                        out=hidden[:],
+                        lhsT=xn_codess[i][:, g, :].bitcast(FP8X4),
+                        lhsT_scale=xn_scaless[i][:, g, :],
+                        rhs=w_codes[:, g, cols].bitcast(FP8X4),
+                        rhs_scale=w_scales[:, g, cols],
+                        start=(g == 0),
+                        stop=(g == PASSES - 1),
+                    )
+                hiddens[i].append(hidden)
+
+        pre_in_0 = BANK - 2 * QK
+
+        def gate_scalar(i):
+            grp, j = divmod(i, TILES_PER_GROUP)
+            if j == 0:
+                qk_stage = stage.tile([P, 2, TILES_PER_GROUP, QK], F32, name="qk_stage")
+                geglu_stage = stage.tile([P, TILES_PER_GROUP, E], F32, name="geglu_stage")
+                stages[grp] = (qk_stage, geglu_stage)
+            hidden_0, hidden_1 = hiddens[i]
+            gelu = work.tile([P, E], F32, name="gelu")
+            nc.scalar.activation(out=gelu[:, 0:pre_in_0], in_=hidden_0[:, 2 * QK : BANK], func=ACT.Gelu)
+            nc.scalar.activation(out=gelu[:, pre_in_0:E], in_=hidden_1[:, 0 : E - pre_in_0], func=ACT.Gelu)
+            nc.scalar.copy(
+                out=stages[grp][0][:, :, j, :], in_=hidden_0[:, 0 : 2 * QK].rearrange("p (o c) -> p o c", o=2)
             )
-            nc.sync.dma_start(
-                out=geglu_rows[rows, :].rearrange("(p j) c -> p j c", j=TILES_PER_GROUP), in_=geglu_stage[:]
+            gelus[i] = gelu
+
+        def gate_vector(i):
+            grp, j = divmod(i, TILES_PER_GROUP)
+            qk_stage, geglu_stage = stages[grp]
+            nc.vector.tensor_tensor(
+                out=geglu_stage[:, j, :], in0=hiddens[i][1][:, E - pre_in_0 : BANK], in1=gelus[i][:], op=ALU.mult
             )
+            if j == TILES_PER_GROUP - 1:
+                rows = slice(grp * GROUP_ROWS, (grp + 1) * GROUP_ROWS)
+                for dram, tile_ap in ((q_rows, qk_stage[:, 0, :, :]), (k_rows, qk_stage[:, 1, :, :]), (geglu_rows, geglu_stage[:])):
+                    nc.sync.dma_start(out=dram[rows, :].rearrange("(p j) c -> p j c", j=TILES_PER_GROUP), in_=tile_ap)
+
+        def in_range(i):
+            return 0 <= i < N_TILES
+
+        slots_per_step = SLOTS // WEIGHT_STEPS
+        for step in range(N_TILES + LAG_GATE):
+            if in_range(step):
+                statistics(step)
+            if in_range(step - LAG_NORMALISE):
+                normalise(step - LAG_NORMALISE)
+            if 1 <= step <= WEIGHT_STEPS:
+                for s in range((step - 1) * slots_per_step, step * slots_per_step):
+                    turn_weights(s)
+                if step % 2 == 0:
+                    quantise_weights(step // 2 - 1)
+            if in_range(step - LAG_TURN):
+                turn(step - LAG_TURN)
+            if in_range(step - LAG_PROJECT):
+                project(step - LAG_PROJECT)
+            if in_range(step - LAG_GATE):
+                gate_vector(step - LAG_GATE)
+            if in_range(step - LAG_TURN):
+                apply_gain(step - LAG_TURN)
+            if in_range(step - LAG_QUANTISE):
+                quantise(step - LAG_QUANTISE)
+            if in_range(step - LAG_PROJECT):
+                gate_scalar(step - LAG_PROJECT)

@@ -29,13 +29,13 @@ TILES_PER_GROUP = 4
 GROUP_ROWS = TILES_PER_GROUP * P
 GROUPS = ROWS // GROUP_ROWS
 N_TILES = ROWS // P
-VECTOR_STATS_EVERY = 3
+TRIPLE = 3
 
-LAG_NORMALISE = 1
-LAG_TURN = 3
-LAG_QUANTISE = 4
-LAG_PROJECT = 5
-LAG_GATE = 6
+LAG_NORMALISE = TRIPLE
+LAG_TURN = 5
+LAG_QUANTISE = 6
+LAG_PROJECT = 7
+LAG_GATE = 8
 WEIGHT_STEPS = 4
 
 FLOPS = 2 * ROWS * W * N
@@ -86,7 +86,7 @@ def tile_latentattentionblock_pa_t_kernel(tc, x, norm_w, expand_w, out_0, out_1,
         make_identity(nc, ident_f32[:])
         ident_bf16 = const.tile([P, P], BF16)
         make_identity(nc, ident_bf16[:])
-        minus_half = const.tile([P, 1], F32)
+        minus_half = const.tile([P, TRIPLE], F32)
         nc.vector.memset(minus_half[:], -0.5)
 
         table_in = const.tile([P, 1], F32)
@@ -100,7 +100,7 @@ def tile_latentattentionblock_pa_t_kernel(tc, x, norm_w, expand_w, out_0, out_1,
         gain_ps = psum.tile([P, P], BF16, tag="turned")
         nc.tensor.transpose(out=gain_ps[:], in_=gain_rows[:], identity=ident_bf16[:])
         gain_t = const.tile([P, W // P], F32)
-        nc.vector.tensor_copy(out=gain_t[:], in_=gain_ps[:, 0 : W // P])
+        nc.vector.tensor_scalar(out=gain_t[:], in0=gain_ps[:, 0 : W // P], scalar1=32.0, scalar2=None, op0=ALU.mult)
 
         w_grouped = const.tile([P, PASSES, N, PACK], BF16, align_bytes=64)
         w_codes = const.tile([P, PASSES, N], U32, align_bytes=64)
@@ -130,16 +130,20 @@ def tile_latentattentionblock_pa_t_kernel(tc, x, norm_w, expand_w, out_0, out_1,
                     in_=w_grouped[:, g, cols, :].rearrange("p n t -> p (n t)"),
                 )
 
-        mean_vars, neg_means, square_sums, centreds, turneds, xn_groupeds = {}, {}, {}, {}, {}, {}
+        mean_vars, means, square_sums, rstds, centreds, turneds, xn_groupeds = {}, {}, {}, {}, {}, {}, {}
         xn_codess, xn_scaless, hiddens, gelus, stages = {}, {}, {}, {}, {}
 
         def x_tile(i):
             return x_groups[i // TILES_PER_GROUP][:, i % TILES_PER_GROUP, :]
 
         def on_vector(i):
-            return i % VECTOR_STATS_EVERY == 1
+            return i % TRIPLE == 1
 
         def statistics(i):
+            m, j = divmod(i, TRIPLE)
+            if j == 0:
+                square_sums[m] = small.tile([P, TRIPLE], F32, name="square_sums")
+                means[m] = small.tile([P, TRIPLE], F32, name="means")
             if on_vector(i):
                 halves = small.tile([P, 2, 6], F32, name="halves")
                 for h in range(2):
@@ -148,38 +152,56 @@ def tile_latentattentionblock_pa_t_kernel(tc, x, norm_w, expand_w, out_0, out_1,
                 nc.vector.bn_aggr(out=mean_var[:], in_=halves[:].rearrange("p h s -> p (h s)"))
                 mean_vars[i] = mean_var
             else:
-                neg_mean = small.tile([P, 1], F32, name="neg_mean")
+                mean = means[m][:, j : j + 1]
                 unread_a = work.tile([P, W], BF16, name="unread_a")
-                nc.scalar.activation(
-                    out=unread_a[:], in_=x_tile(i), func=ACT.Copy, scale=-1.0 / W, accum_out=neg_mean[:]
-                )
+                nc.scalar.activation(out=unread_a[:], in_=x_tile(i), func=ACT.Copy, scale=1.0 / W, accum_out=mean)
                 unread_b = work.tile([P, W], BF16, name="unread_b")
-                square_sum = small.tile([P, 1], F32, name="square_sum")
                 nc.scalar.activation(
-                    out=unread_b[:], in_=x_tile(i), func=ACT.Square, bias=neg_mean[:], accum_out=square_sum[:]
+                    out=unread_b[:],
+                    in_=x_tile(i),
+                    func=ACT.Square,
+                    scale=-1.0,
+                    bias=mean,
+                    accum_out=square_sums[m][:, j : j + 1],
                 )
-                neg_means[i] = neg_mean
-                square_sums[i] = square_sum
+
+        def rstd_triple(m):
+            count = min(TRIPLE, N_TILES - m * TRIPLE)
+            var_eps = small.tile([P, TRIPLE], F32, name="var_eps")
+            nc.gpsimd.tensor_scalar(
+                out=var_eps[:, 0:count:2],
+                in0=square_sums[m][:, 0:count:2],
+                scalar1=1.0,
+                scalar2=W * EPS,
+                op0=ALU.mult,
+                op1=ALU.add,
+            )
+            nc.gpsimd.tensor_scalar(
+                out=var_eps[:, 1:2],
+                in0=mean_vars[m * TRIPLE + 1][:, 1:2],
+                scalar1=float(W),
+                scalar2=W * EPS,
+                op0=ALU.mult,
+                op1=ALU.add,
+            )
+            rstds[m] = small.tile([P, TRIPLE], F32, name="rstd")
+            nc.gpsimd.tensor_tensor(
+                out=rstds[m][:, 0:count], in0=var_eps[:, 0:count], in1=minus_half[:, 0:count], op=ALU.pow
+            )
 
         def normalise(i):
-            var_eps = small.tile([P, 1], F32, name="var_eps")
-            if on_vector(i):
-                neg_means[i] = small.tile([P, 1], F32, name="neg_mean")
-                nc.gpsimd.tensor_scalar(
-                    out=neg_means[i][:], in0=mean_vars[i][:, 0:1], scalar1=-1.0, scalar2=0.0, op0=ALU.mult, op1=ALU.add
-                )
-                nc.gpsimd.tensor_scalar(
-                    out=var_eps[:], in0=mean_vars[i][:, 1:2], scalar1=1.0, scalar2=EPS, op0=ALU.mult, op1=ALU.add
-                )
-            else:
-                nc.gpsimd.tensor_scalar(
-                    out=var_eps[:], in0=square_sums[i][:], scalar1=1.0 / W, scalar2=EPS, op0=ALU.mult, op1=ALU.add
-                )
-            rstd = small.tile([P, 1], F32, name="rstd")
-            nc.gpsimd.tensor_tensor(out=rstd[:], in0=var_eps[:], in1=minus_half[:], op=ALU.pow)
+            m, j = divmod(i, TRIPLE)
+            if j == 0:
+                rstd_triple(m)
+            mean = mean_vars[i][:, 0:1] if on_vector(i) else means[m][:, j : j + 1]
             centred = work.tile([P, W], F32, name="centred", bufs=4)
             nc.gpsimd.tensor_scalar(
-                out=centred[:], in0=x_tile(i), scalar1=neg_means[i][:], scalar2=rstd[:], op0=ALU.add, op1=ALU.mult
+                out=centred[:],
+                in0=x_tile(i),
+                scalar1=mean,
+                scalar2=rstds[m][:, j : j + 1],
+                op0=ALU.subtract,
+                op1=ALU.mult,
             )
             centreds[i] = centred
 

@@ -130,7 +130,7 @@ def tile_latentattentionblock_pa_t_kernel(tc, x, norm_w, expand_w, out_0, out_1,
                     in_=w_grouped[:, g, cols, :].rearrange("p n t -> p (n t)"),
                 )
 
-        mean_vars, means, square_sums, rstds, centreds, turneds, xn_groupeds = {}, {}, {}, {}, {}, {}, {}
+        mean_vars, neg_means, square_sums, rstds, centreds, turneds, xn_groupeds = {}, {}, {}, {}, {}, {}, {}
         xn_codess, xn_scaless, hiddens, gelus, stages = {}, {}, {}, {}, {}
 
         def x_tile(i):
@@ -143,7 +143,7 @@ def tile_latentattentionblock_pa_t_kernel(tc, x, norm_w, expand_w, out_0, out_1,
             m, j = divmod(i, TRIPLE)
             if j == 0:
                 square_sums[m] = small.tile([P, TRIPLE], F32, name="square_sums")
-                means[m] = small.tile([P, TRIPLE], F32, name="means")
+                neg_means[m] = small.tile([P, TRIPLE], F32, name="neg_means")
             if on_vector(i):
                 halves = small.tile([P, 2, 6], F32, name="halves")
                 for h in range(2):
@@ -152,16 +152,15 @@ def tile_latentattentionblock_pa_t_kernel(tc, x, norm_w, expand_w, out_0, out_1,
                 nc.vector.bn_aggr(out=mean_var[:], in_=halves[:].rearrange("p h s -> p (h s)"))
                 mean_vars[i] = mean_var
             else:
-                mean = means[m][:, j : j + 1]
+                neg_mean = neg_means[m][:, j : j + 1]
                 unread_a = work.tile([P, W], BF16, name="unread_a")
-                nc.scalar.activation(out=unread_a[:], in_=x_tile(i), func=ACT.Copy, scale=1.0 / W, accum_out=mean)
+                nc.scalar.activation(out=unread_a[:], in_=x_tile(i), func=ACT.Copy, scale=-1.0 / W, accum_out=neg_mean)
                 unread_b = work.tile([P, W], BF16, name="unread_b")
                 nc.scalar.activation(
                     out=unread_b[:],
                     in_=x_tile(i),
                     func=ACT.Square,
-                    scale=-1.0,
-                    bias=mean,
+                    bias=neg_mean,
                     accum_out=square_sums[m][:, j : j + 1],
                 )
 
@@ -184,6 +183,14 @@ def tile_latentattentionblock_pa_t_kernel(tc, x, norm_w, expand_w, out_0, out_1,
                 op0=ALU.mult,
                 op1=ALU.add,
             )
+            nc.gpsimd.tensor_scalar(
+                out=neg_means[m][:, 1:2],
+                in0=mean_vars[m * TRIPLE + 1][:, 0:1],
+                scalar1=-1.0,
+                scalar2=0.0,
+                op0=ALU.mult,
+                op1=ALU.add,
+            )
             rstds[m] = small.tile([P, TRIPLE], F32, name="rstd")
             nc.gpsimd.tensor_tensor(
                 out=rstds[m][:, 0:count], in0=var_eps[:, 0:count], in1=minus_half[:, 0:count], op=ALU.pow
@@ -193,14 +200,13 @@ def tile_latentattentionblock_pa_t_kernel(tc, x, norm_w, expand_w, out_0, out_1,
             m, j = divmod(i, TRIPLE)
             if j == 0:
                 rstd_triple(m)
-            mean = mean_vars[i][:, 0:1] if on_vector(i) else means[m][:, j : j + 1]
             centred = work.tile([P, W], F32, name="centred", bufs=4)
             nc.gpsimd.tensor_scalar(
                 out=centred[:],
                 in0=x_tile(i),
-                scalar1=mean,
+                scalar1=neg_means[m][:, j : j + 1],
                 scalar2=rstds[m][:, j : j + 1],
-                op0=ALU.subtract,
+                op0=ALU.add,
                 op1=ALU.mult,
             )
             centreds[i] = centred

@@ -29,14 +29,16 @@ TILES_PER_GROUP = 4
 GROUP_ROWS = TILES_PER_GROUP * P
 GROUPS = ROWS // GROUP_ROWS
 N_TILES = ROWS // P
+VECTOR_HEAD = 5
 TRIPLE = 3
+CUT = 344
 
-LAG_NORMALISE = TRIPLE
-LAG_TURN = 5
-LAG_QUANTISE = 6
-LAG_PROJECT = 7
-LAG_GATE = 8
-WEIGHT_STEPS = 4
+LAG_TURN = 1
+LAG_GAIN = 2
+LAG_QUANTISE = 3
+LAG_PROJECT = 4
+LAG_GATE = 5
+FIRST_STEP = -1
 
 FLOPS = 2 * ROWS * W * N
 
@@ -97,18 +99,22 @@ def tile_latentattentionblock_pa_t_kernel(tc, x, norm_w, expand_w, out_0, out_1,
         gain_rows = const.tile([P, P], BF16)
         nc.vector.memset(gain_rows[:], 0.0)
         nc.scalar.dma_start(out=gain_rows[0 : W // P, :], in_=norm_w.rearrange("(c p) -> c p", p=P))
-        gain_ps = psum.tile([P, P], BF16, tag="turned")
-        nc.tensor.transpose(out=gain_ps[:], in_=gain_rows[:], identity=ident_bf16[:])
         gain_t = const.tile([P, W // P], F32)
-        nc.vector.tensor_scalar(out=gain_t[:], in0=gain_ps[:, 0 : W // P], scalar1=32.0, scalar2=None, op0=ALU.mult)
+
+        def turn_gain():
+            gain_ps = psum.tile([P, P], BF16, tag="turned")
+            nc.tensor.transpose(out=gain_ps[:], in_=gain_rows[:], identity=ident_bf16[:])
+            nc.vector.tensor_scalar(
+                out=gain_t[:], in0=gain_ps[:, 0 : W // P], scalar1=32.0, scalar2=None, op0=ALU.mult
+            )
 
         w_grouped = const.tile([P, PASSES, N, PACK], BF16, align_bytes=64)
         w_codes = const.tile([P, PASSES, N], U32, align_bytes=64)
         w_scales = const.tile([P, PASSES, N], U8, align_bytes=64)
 
-        def turn_weights(s):
+        def turn_weights(s, vector_takes):
             for g in range(PASSES):
-                w_turned = psum.tile([P, PACK, P], BF16, tag="turned")
+                w_turned = psum.tile([P, PACK, P], BF16, tag="hidden", name="w_turned")
                 for t in range(PACK):
                     k0 = g * K_PASS + t * P
                     nc.tensor.transpose(
@@ -116,7 +122,7 @@ def tile_latentattentionblock_pa_t_kernel(tc, x, norm_w, expand_w, out_0, out_1,
                     )
                 dst = w_grouped[:, g, s * P : (s + 1) * P, :]
                 src = w_turned[:].rearrange("p t n -> p n t")
-                if g == 0:
+                if g in vector_takes:
                     nc.vector.tensor_copy(out=dst, in_=src)
                 else:
                     nc.scalar.copy(out=dst, in_=src)
@@ -130,62 +136,110 @@ def tile_latentattentionblock_pa_t_kernel(tc, x, norm_w, expand_w, out_0, out_1,
                     in_=w_grouped[:, g, cols, :].rearrange("p n t -> p (n t)"),
                 )
 
-        mean_vars, neg_means, square_sums, rstds, centreds, turneds, xn_groupeds = {}, {}, {}, {}, {}, {}, {}
+        rstd_groups = [[i] for i in range(VECTOR_HEAD)]
+        for i in range(VECTOR_HEAD, N_TILES, TRIPLE):
+            rstd_groups.append([i + 1, i, i + 2])
+        place = {}
+        neg_means, sums, mean_vars, rstds, parts, bn_parts = {}, {}, {}, {}, {}, {}
+        for m, members in enumerate(rstd_groups):
+            for column, i in enumerate(members):
+                place[i] = (m, column)
+        centreds, turneds, xn_groupeds = {}, {}, {}
         xn_codess, xn_scaless, hiddens, gelus, stages = {}, {}, {}, {}, {}
 
         def x_tile(i):
             return x_groups[i // TILES_PER_GROUP][:, i % TILES_PER_GROUP, :]
 
-        def on_vector(i):
-            return i % TRIPLE == 1
+        def column_of(tiles, i):
+            m, column = place[i]
+            return tiles[m][:, column : column + 1]
 
-        def statistics(i):
-            m, j = divmod(i, TRIPLE)
-            if j == 0:
-                square_sums[m] = small.tile([P, TRIPLE], F32, name="square_sums")
-                neg_means[m] = small.tile([P, TRIPLE], F32, name="neg_means")
-            if on_vector(i):
-                halves = small.tile([P, 2, 6], F32, name="halves")
-                for h in range(2):
-                    nc.vector.bn_stats(out=halves[:, h, :], in_=x_tile(i)[:, h * 512 : (h + 1) * 512])
-                mean_var = small.tile([P, 2], F32, name="mean_var")
-                nc.vector.bn_aggr(out=mean_var[:], in_=halves[:].rearrange("p h s -> p (h s)"))
-                mean_vars[i] = mean_var
+        def open_group(m):
+            neg_means[m] = small.tile([P, TRIPLE], F32, name="neg_means")
+            sums[m] = small.tile([P, TRIPLE], F32, name="sums")
+            mean_vars[m] = small.tile([P, 2, 2], F32, name="mean_vars")
+
+        def vector_part(i, part, c0, c1):
+            if part == 0:
+                bn_parts[i] = small.tile([P, TRIPLE, 6], F32, name="bn_parts")
+            nc.vector.bn_stats(out=bn_parts[i][:, part, :], in_=x_tile(i)[:, c0:c1])
+
+        def vector_sum(i, n_parts):
+            m, column = place[i]
+            nc.vector.bn_aggr(
+                out=mean_vars[m][:, column, :], in_=bn_parts[i][:, 0:n_parts, :].rearrange("p h s -> p (h s)")
+            )
+
+        def scalar_mean(i, c0, c1, total):
+            unread_a = work.tile([P, W], BF16, name="unread_a")
+            nc.scalar.activation(
+                out=unread_a[:, c0:c1], in_=x_tile(i)[:, c0:c1], func=ACT.Copy, scale=-1.0 / W, accum_out=total
+            )
+
+        def scalar_squares(i, c0, c1, total):
+            unread_b = work.tile([P, W], BF16, name="unread_b")
+            nc.scalar.activation(
+                out=unread_b[:, c0:c1],
+                in_=x_tile(i)[:, c0:c1],
+                func=ACT.Square,
+                bias=column_of(neg_means, i),
+                accum_out=total,
+            )
+
+        def scalar_add(out, a, b):
+            nc.scalar.activation(out=out, in_=a, func=ACT.Identity, bias=b)
+
+        def head_statistics(i):
+            m, column = place[i]
+            if column == 0:
+                open_group(m)
+            for h in range(2):
+                vector_part(i, h, h * 512, (h + 1) * 512)
+
+        def triple_scalar(first, third):
+            a, b = first, first + 2
+            if third == 0:
+                open_group(place[a][0])
+                parts[first] = small.tile([P, 4], F32, name="parts")
+                scalar_mean(a, 0, W, column_of(neg_means, a))
+                scalar_mean(b, 0, CUT, parts[first][:, 0:1])
+            elif third == 1:
+                scalar_mean(b, CUT, W, parts[first][:, 1:2])
+                scalar_squares(a, 0, W - CUT, parts[first][:, 2:3])
+                scalar_add(column_of(neg_means, b), parts[first][:, 0:1], parts[first][:, 1:2])
             else:
-                neg_mean = neg_means[m][:, j : j + 1]
-                unread_a = work.tile([P, W], BF16, name="unread_a")
-                nc.scalar.activation(out=unread_a[:], in_=x_tile(i), func=ACT.Copy, scale=-1.0 / W, accum_out=neg_mean)
-                unread_b = work.tile([P, W], BF16, name="unread_b")
-                nc.scalar.activation(
-                    out=unread_b[:],
-                    in_=x_tile(i),
-                    func=ACT.Square,
-                    bias=neg_mean,
-                    accum_out=square_sums[m][:, j : j + 1],
-                )
+                scalar_squares(a, W - CUT, W, parts[first][:, 3:4])
+                scalar_squares(b, 0, W, column_of(sums, b))
+                scalar_add(column_of(sums, a), parts[first][:, 2:3], parts[first][:, 3:4])
 
-        def rstd_triple(m):
-            count = min(TRIPLE, N_TILES - m * TRIPLE)
+        def triple_vector(first, third):
+            edges = (0, CUT, (CUT + W) // 2, W)
+            vector_part(first + 1, third, edges[third], edges[third + 1])
+
+        def find_rstd(m):
+            count = len(rstd_groups[m])
+            by_vector = 1 if count == TRIPLE else count
             var_eps = small.tile([P, TRIPLE], F32, name="var_eps")
             nc.gpsimd.tensor_scalar(
-                out=var_eps[:, 0:count:2],
-                in0=square_sums[m][:, 0:count:2],
-                scalar1=1.0,
-                scalar2=W * EPS,
-                op0=ALU.mult,
-                op1=ALU.add,
-            )
-            nc.gpsimd.tensor_scalar(
-                out=var_eps[:, 1:2],
-                in0=mean_vars[m * TRIPLE + 1][:, 1:2],
+                out=var_eps[:, 0:by_vector],
+                in0=mean_vars[m][:, 0:by_vector, 1],
                 scalar1=float(W),
                 scalar2=W * EPS,
                 op0=ALU.mult,
                 op1=ALU.add,
             )
+            if by_vector < count:
+                nc.gpsimd.tensor_scalar(
+                    out=var_eps[:, by_vector:count],
+                    in0=sums[m][:, by_vector:count],
+                    scalar1=1.0,
+                    scalar2=W * EPS,
+                    op0=ALU.mult,
+                    op1=ALU.add,
+                )
             nc.gpsimd.tensor_scalar(
-                out=neg_means[m][:, 1:2],
-                in0=mean_vars[m * TRIPLE + 1][:, 0:1],
+                out=neg_means[m][:, 0:by_vector],
+                in0=mean_vars[m][:, 0:by_vector, 0],
                 scalar1=-1.0,
                 scalar2=0.0,
                 op0=ALU.mult,
@@ -197,15 +251,15 @@ def tile_latentattentionblock_pa_t_kernel(tc, x, norm_w, expand_w, out_0, out_1,
             )
 
         def normalise(i):
-            m, j = divmod(i, TRIPLE)
-            if j == 0:
-                rstd_triple(m)
+            m, column = place[i]
+            if i == min(rstd_groups[m]):
+                find_rstd(m)
             centred = work.tile([P, W], F32, name="centred", bufs=4)
             nc.gpsimd.tensor_scalar(
                 out=centred[:],
                 in0=x_tile(i),
-                scalar1=neg_means[m][:, j : j + 1],
-                scalar2=rstds[m][:, j : j + 1],
+                scalar1=column_of(neg_means, i),
+                scalar2=column_of(rstds, i),
                 op0=ALU.add,
                 op1=ALU.mult,
             )
@@ -291,26 +345,39 @@ def tile_latentattentionblock_pa_t_kernel(tc, x, norm_w, expand_w, out_0, out_1,
         def in_range(i):
             return 0 <= i < N_TILES
 
-        slots_per_step = SLOTS // WEIGHT_STEPS
-        for step in range(N_TILES + LAG_GATE):
-            if in_range(step):
-                statistics(step)
-            if in_range(step - LAG_NORMALISE):
-                normalise(step - LAG_NORMALISE)
-            if 1 <= step <= WEIGHT_STEPS:
-                for s in range((step - 1) * slots_per_step, step * slots_per_step):
-                    turn_weights(s)
-                if step % 2 == 0:
-                    quantise_weights(step // 2 - 1)
-            if in_range(step - LAG_TURN):
-                turn(step - LAG_TURN)
-            if in_range(step - LAG_PROJECT):
-                project(step - LAG_PROJECT)
-            if in_range(step - LAG_GATE):
-                gate_vector(step - LAG_GATE)
-            if in_range(step - LAG_TURN):
-                apply_gain(step - LAG_TURN)
+        for step in range(FIRST_STEP, N_TILES + LAG_GATE):
+            m, third = divmod(step + TRIPLE - VECTOR_HEAD, TRIPLE)
+            first = VECTOR_HEAD + m * TRIPLE
+
             if in_range(step - LAG_QUANTISE):
                 quantise(step - LAG_QUANTISE)
+            if third == 0 and m > 0 and first - TRIPLE < N_TILES:
+                vector_sum(first - TRIPLE + 1, TRIPLE)
+            if in_range(step):
+                normalise(step)
+            if in_range(step - LAG_PROJECT):
+                project(step - LAG_PROJECT)
+            if in_range(step - LAG_TURN):
+                turn(step - LAG_TURN)
+            if step + 1 < VECTOR_HEAD:
+                head_statistics(step + 1)
+            if step == 0:
+                turn_gain()
+            if step < 3:
+                slot = 2 * (step - FIRST_STEP)
+                turn_weights(slot, ())
+                turn_weights(slot + 1, (1,) if step < 2 else ())
+
+            if in_range(step - LAG_GATE):
+                gate_vector(step - LAG_GATE)
+            if in_range(step - LAG_GAIN):
+                apply_gain(step - LAG_GAIN)
+            if m >= 0 and first < N_TILES:
+                triple_vector(first, third)
+                triple_scalar(first, third)
+            if step + 1 < VECTOR_HEAD:
+                vector_sum(step + 1, 2)
+            if step in (2, 3):
+                quantise_weights(step - 2)
             if in_range(step - LAG_PROJECT):
                 gate_scalar(step - LAG_PROJECT)

@@ -140,7 +140,7 @@ def tile_latentattentionblock_pa_t_kernel(tc, x, norm_w, expand_w, out_0, out_1,
         for i in range(VECTOR_HEAD, N_TILES, TRIPLE):
             rstd_groups.append([i + 1, i, i + 2])
         place = {}
-        neg_means, sums, mean_vars, rstds, parts, bn_parts = {}, {}, {}, {}, {}, {}
+        neg_means, sums, mean_vars, rstds, parts, bn_parts, shifts = {}, {}, {}, {}, {}, {}, {}
         for m, members in enumerate(rstd_groups):
             for column, i in enumerate(members):
                 place[i] = (m, column)
@@ -237,31 +237,34 @@ def tile_latentattentionblock_pa_t_kernel(tc, x, norm_w, expand_w, out_0, out_1,
                     op0=ALU.mult,
                     op1=ALU.add,
                 )
-            nc.gpsimd.tensor_scalar(
-                out=neg_means[m][:, 0:by_vector],
-                in0=mean_vars[m][:, 0:by_vector, 0],
-                scalar1=-1.0,
-                scalar2=0.0,
-                op0=ALU.mult,
-                op1=ALU.add,
-            )
             rstds[m] = small.tile([P, TRIPLE], F32, name="rstd")
             nc.gpsimd.tensor_tensor(
                 out=rstds[m][:, 0:count], in0=var_eps[:, 0:count], in1=minus_half[:, 0:count], op=ALU.pow
             )
 
-        def normalise(i):
+        def find_shift(i):
             m, column = place[i]
-            if i == min(rstd_groups[m]):
-                find_rstd(m)
+            shifts[i] = small.tile([P, 1], F32, name="shift")
+            by_scalar = len(rstd_groups[m]) == TRIPLE and column > 0
+            mean = column_of(neg_means, i) if by_scalar else mean_vars[m][:, column, 0:1]
+            nc.vector.scalar_tensor_tensor(
+                out=shifts[i][:],
+                in0=mean,
+                scalar=1.0 if by_scalar else -1.0,
+                in1=column_of(rstds, i),
+                op0=ALU.mult,
+                op1=ALU.mult,
+            )
+
+        def normalise(i):
             centred = work.tile([P, W], F32, name="centred", bufs=4)
             nc.gpsimd.tensor_scalar(
                 out=centred[:],
                 in0=x_tile(i),
-                scalar1=column_of(neg_means, i),
-                scalar2=column_of(rstds, i),
-                op0=ALU.add,
-                op1=ALU.mult,
+                scalar1=column_of(rstds, i),
+                scalar2=shifts[i][:],
+                op0=ALU.mult,
+                op1=ALU.add,
             )
             centreds[i] = centred
 
@@ -346,15 +349,17 @@ def tile_latentattentionblock_pa_t_kernel(tc, x, norm_w, expand_w, out_0, out_1,
             return 0 <= i < N_TILES
 
         for step in range(FIRST_STEP, N_TILES + LAG_GATE):
-            m, third = divmod(step + TRIPLE - VECTOR_HEAD, TRIPLE)
+            m, third = divmod(step + TRIPLE + 1 - VECTOR_HEAD, TRIPLE)
             first = VECTOR_HEAD + m * TRIPLE
 
             if in_range(step - LAG_QUANTISE):
                 quantise(step - LAG_QUANTISE)
+            if in_range(step):
+                find_shift(step)
+                normalise(step)
             if third == 0 and m > 0 and first - TRIPLE < N_TILES:
                 vector_sum(first - TRIPLE + 1, TRIPLE)
-            if in_range(step):
-                normalise(step)
+                find_rstd(place[first - TRIPLE][0])
             if in_range(step - LAG_PROJECT):
                 project(step - LAG_PROJECT)
             if in_range(step - LAG_TURN):
@@ -370,13 +375,14 @@ def tile_latentattentionblock_pa_t_kernel(tc, x, norm_w, expand_w, out_0, out_1,
 
             if in_range(step - LAG_GATE):
                 gate_vector(step - LAG_GATE)
+            if step + 1 < VECTOR_HEAD:
+                vector_sum(step + 1, 2)
+                find_rstd(place[step + 1][0])
             if in_range(step - LAG_GAIN):
                 apply_gain(step - LAG_GAIN)
             if m >= 0 and first < N_TILES:
                 triple_vector(first, third)
                 triple_scalar(first, third)
-            if step + 1 < VECTOR_HEAD:
-                vector_sum(step + 1, 2)
             if step in (2, 3):
                 quantise_weights(step - 2)
             if in_range(step - LAG_PROJECT):

@@ -38,6 +38,7 @@ LAG_GAIN = 2
 LAG_QUANTISE = 3
 LAG_PROJECT = 4
 LAG_GATE = 5
+RSTD_AHEAD = 2
 FIRST_STEP = -1
 
 FLOPS = 2 * ROWS * W * N
@@ -349,7 +350,7 @@ def tile_latentattentionblock_pa_t_kernel(tc, x, norm_w, expand_w, out_0, out_1,
             return 0 <= i < N_TILES
 
         for step in range(FIRST_STEP, N_TILES + LAG_GATE):
-            m, third = divmod(step + TRIPLE + 1 - VECTOR_HEAD, TRIPLE)
+            m, third = divmod(step + TRIPLE + RSTD_AHEAD - VECTOR_HEAD, TRIPLE)
             first = VECTOR_HEAD + m * TRIPLE
 
             if in_range(step - LAG_QUANTISE):

@@ -31,14 +31,13 @@ GROUPS = ROWS // GROUP_ROWS
 N_TILES = ROWS // P
 VECTOR_HEAD = 5
 TRIPLE = 3
-CUT = 344
 
 LAG_TURN = 1
 LAG_GAIN = 2
 LAG_QUANTISE = 3
 LAG_PROJECT = 4
 LAG_GATE = 5
-RSTD_AHEAD = 2
+RSTD_AHEAD = 1
 FIRST_STEP = -1
 
 FLOPS = 2 * ROWS * W * N
@@ -58,6 +57,7 @@ def tile_latentattentionblock_pa_t_kernel(tc, x, norm_w, expand_w, out_0, out_1,
         small = pools.enter_context(tc.tile_pool(name="small", bufs=4))
         work = pools.enter_context(tc.tile_pool(name="work", bufs=3))
         stage = pools.enter_context(tc.tile_pool(name="stage", bufs=2))
+        ring = pools.enter_context(tc.tile_pool(name="ring", bufs=1))
         psum = pools.enter_context(tc.psum_pool(name="psum", bufs=4))
 
         x_groups = []
@@ -82,13 +82,13 @@ def tile_latentattentionblock_pa_t_kernel(tc, x, norm_w, expand_w, out_0, out_1,
         load_x(0, 2, 4)
         load_w(2, 5, 2 * QK + E)
         load_w(5, 8, 2 * QK)
-        for grp in range(1, GROUPS):
+        load_x(1, 0, 1)
+        load_x(1, 1, TILES_PER_GROUP)
+        for grp in range(2, GROUPS):
             load_x(grp, 0, TILES_PER_GROUP)
 
         ident_f32 = const.tile([P, P], F32)
         make_identity(nc, ident_f32[:])
-        ident_bf16 = const.tile([P, P], BF16)
-        make_identity(nc, ident_bf16[:])
         minus_half = const.tile([P, TRIPLE], F32)
         nc.vector.memset(minus_half[:], -0.5)
 
@@ -97,36 +97,30 @@ def tile_latentattentionblock_pa_t_kernel(tc, x, norm_w, expand_w, out_0, out_1,
         table_out = const.tile([P, 1], F32)
         nc.scalar.activation(out=table_out[:], in_=table_in[:], func=ACT.Gelu)
 
-        gain_rows = const.tile([P, P], BF16)
+        gain_rows = const.tile([P, 2 * P], BF16)
         nc.vector.memset(gain_rows[:], 0.0)
-        nc.scalar.dma_start(out=gain_rows[0 : W // P, :], in_=norm_w.rearrange("(c p) -> c p", p=P))
+        nc.scalar.dma_start(out=gain_rows[0 : W // (2 * P), :], in_=norm_w.rearrange("(c k) -> c k", k=2 * P))
         gain_t = const.tile([P, W // P], F32)
 
         def turn_gain():
-            gain_ps = psum.tile([P, P], BF16, tag="turned")
-            nc.tensor.transpose(out=gain_ps[:], in_=gain_rows[:], identity=ident_bf16[:])
+            gain_ps = psum.tile([P, P], F32, tag="turned")
+            nc.tensor.transpose(out=gain_ps[:], in_=gain_rows[:].bitcast(F32), identity=ident_f32[:])
             nc.vector.tensor_scalar(
-                out=gain_t[:], in0=gain_ps[:, 0 : W // P], scalar1=32.0, scalar2=None, op0=ALU.mult
+                out=gain_t[:], in0=gain_ps[:].bitcast(BF16)[:, 0 : W // P], scalar1=32.0, scalar2=None, op0=ALU.mult
             )
 
         w_grouped = const.tile([P, PASSES, N, PACK], BF16, align_bytes=64)
         w_codes = const.tile([P, PASSES, N], U32, align_bytes=64)
         w_scales = const.tile([P, PASSES, N], U8, align_bytes=64)
 
-        def turn_weights(s, vector_takes):
-            for g in range(PASSES):
-                w_turned = psum.tile([P, PACK, P], BF16, tag="hidden", name="w_turned")
-                for t in range(PACK):
-                    k0 = g * K_PASS + t * P
-                    nc.tensor.transpose(
-                        out=w_turned[:, t, :], in_=w_rows[:, s, k0 : k0 + P], identity=ident_bf16[:]
-                    )
-                dst = w_grouped[:, g, s * P : (s + 1) * P, :]
-                src = w_turned[:].rearrange("p t n -> p n t")
-                if g in vector_takes:
-                    nc.vector.tensor_copy(out=dst, in_=src)
-                else:
-                    nc.scalar.copy(out=dst, in_=src)
+        def turn_weights(s):
+            w_turned = psum.tile([P, PACK, P], F32, tag="hidden", name="w_turned")
+            words = w_rows[:, s, :].bitcast(F32)
+            for c in range(PACK):
+                nc.tensor.transpose(out=w_turned[:, c, :], in_=words[:, c * P : (c + 1) * P], identity=ident_f32[:])
+            dst = w_grouped[:, :, s * P : (s + 1) * P, :].bitcast(F32)
+            src = w_turned[:].rearrange("p (g u) n -> p g n u", g=PASSES)
+            nc.scalar.copy(out=dst, in_=src)
 
         def quantise_weights(bank):
             cols = slice(bank * BANK, (bank + 1) * BANK)
@@ -137,11 +131,11 @@ def tile_latentattentionblock_pa_t_kernel(tc, x, norm_w, expand_w, out_0, out_1,
                     in_=w_grouped[:, g, cols, :].rearrange("p n t -> p (n t)"),
                 )
 
-        rstd_groups = [[i] for i in range(VECTOR_HEAD)]
+        rstd_groups = [[0], [1, 2], [3, 4]]
         for i in range(VECTOR_HEAD, N_TILES, TRIPLE):
             rstd_groups.append([i + 1, i, i + 2])
         place = {}
-        neg_means, sums, mean_vars, rstds, parts, bn_parts, shifts = {}, {}, {}, {}, {}, {}, {}
+        neg_means, sums, mean_vars, rstds, halves = {}, {}, {}, {}, {}
         for m, members in enumerate(rstd_groups):
             for column, i in enumerate(members):
                 place[i] = (m, column)
@@ -160,62 +154,46 @@ def tile_latentattentionblock_pa_t_kernel(tc, x, norm_w, expand_w, out_0, out_1,
             sums[m] = small.tile([P, TRIPLE], F32, name="sums")
             mean_vars[m] = small.tile([P, 2, 2], F32, name="mean_vars")
 
-        def vector_part(i, part, c0, c1):
-            if part == 0:
-                bn_parts[i] = small.tile([P, TRIPLE, 6], F32, name="bn_parts")
-            nc.vector.bn_stats(out=bn_parts[i][:, part, :], in_=x_tile(i)[:, c0:c1])
+        def vector_half(i, half):
+            if half == 0:
+                halves[i] = small.tile([P, 2, 6], F32, name="halves")
+            nc.vector.bn_stats(out=halves[i][:, half, :], in_=x_tile(i)[:, half * 512 : (half + 1) * 512])
 
-        def vector_sum(i, n_parts):
+        def vector_sum(i):
             m, column = place[i]
-            nc.vector.bn_aggr(
-                out=mean_vars[m][:, column, :], in_=bn_parts[i][:, 0:n_parts, :].rearrange("p h s -> p (h s)")
-            )
+            nc.vector.bn_aggr(out=mean_vars[m][:, column, :], in_=halves[i][:].rearrange("p h s -> p (h s)"))
 
-        def scalar_mean(i, c0, c1, total):
+        def scalar_mean(i):
             unread_a = work.tile([P, W], BF16, name="unread_a")
             nc.scalar.activation(
-                out=unread_a[:, c0:c1], in_=x_tile(i)[:, c0:c1], func=ACT.Copy, scale=-1.0 / W, accum_out=total
+                out=unread_a[:], in_=x_tile(i), func=ACT.Copy, scale=-1.0 / W, accum_out=column_of(neg_means, i)
             )
 
-        def scalar_squares(i, c0, c1, total):
+        def scalar_squares(i):
             unread_b = work.tile([P, W], BF16, name="unread_b")
             nc.scalar.activation(
-                out=unread_b[:, c0:c1],
-                in_=x_tile(i)[:, c0:c1],
+                out=unread_b[:],
+                in_=x_tile(i),
                 func=ACT.Square,
                 bias=column_of(neg_means, i),
-                accum_out=total,
+                accum_out=column_of(sums, i),
             )
 
-        def scalar_add(out, a, b):
-            nc.scalar.activation(out=out, in_=a, func=ACT.Identity, bias=b)
-
         def head_statistics(i):
-            m, column = place[i]
-            if column == 0:
-                open_group(m)
-            for h in range(2):
-                vector_part(i, h, h * 512, (h + 1) * 512)
+            if place[i][1] == 0:
+                open_group(place[i][0])
+            vector_half(i, 0)
+            vector_half(i, 1)
 
-        def triple_scalar(first, third):
-            a, b = first, first + 2
+        def triple_statistics(first, third):
             if third == 0:
-                open_group(place[a][0])
-                parts[first] = small.tile([P, 4], F32, name="parts")
-                scalar_mean(a, 0, W, column_of(neg_means, a))
-                scalar_mean(b, 0, CUT, parts[first][:, 0:1])
-            elif third == 1:
-                scalar_mean(b, CUT, W, parts[first][:, 1:2])
-                scalar_squares(a, 0, W - CUT, parts[first][:, 2:3])
-                scalar_add(column_of(neg_means, b), parts[first][:, 0:1], parts[first][:, 1:2])
+                open_group(place[first][0])
+                scalar_mean(first)
+                scalar_mean(first + 2)
             else:
-                scalar_squares(a, W - CUT, W, parts[first][:, 3:4])
-                scalar_squares(b, 0, W, column_of(sums, b))
-                scalar_add(column_of(sums, a), parts[first][:, 2:3], parts[first][:, 3:4])
-
-        def triple_vector(first, third):
-            edges = (0, CUT, (CUT + W) // 2, W)
-            vector_part(first + 1, third, edges[third], edges[third + 1])
+                half = third - 1
+                vector_half(first + 1, half)
+                scalar_squares(first + 2 * half)
 
         def find_rstd(m):
             count = len(rstd_groups[m])
@@ -238,34 +216,28 @@ def tile_latentattentionblock_pa_t_kernel(tc, x, norm_w, expand_w, out_0, out_1,
                     op0=ALU.mult,
                     op1=ALU.add,
                 )
+            nc.gpsimd.tensor_scalar(
+                out=neg_means[m][:, 0:by_vector],
+                in0=mean_vars[m][:, 0:by_vector, 0],
+                scalar1=-1.0,
+                scalar2=0.0,
+                op0=ALU.mult,
+                op1=ALU.add,
+            )
             rstds[m] = small.tile([P, TRIPLE], F32, name="rstd")
             nc.gpsimd.tensor_tensor(
                 out=rstds[m][:, 0:count], in0=var_eps[:, 0:count], in1=minus_half[:, 0:count], op=ALU.pow
             )
 
-        def find_shift(i):
-            m, column = place[i]
-            shifts[i] = small.tile([P, 1], F32, name="shift")
-            by_scalar = len(rstd_groups[m]) == TRIPLE and column > 0
-            mean = column_of(neg_means, i) if by_scalar else mean_vars[m][:, column, 0:1]
-            nc.vector.scalar_tensor_tensor(
-                out=shifts[i][:],
-                in0=mean,
-                scalar=1.0 if by_scalar else -1.0,
-                in1=column_of(rstds, i),
-                op0=ALU.mult,
-                op1=ALU.mult,
-            )
-
         def normalise(i):
-            centred = work.tile([P, W], F32, name="centred", bufs=4)
+            centred = ring.tile([P, W], F32, name="centred", tag="centred_%d" % (i % 3), offset=(i % 3) * W * 4, align_bytes=64)
             nc.gpsimd.tensor_scalar(
-                out=centred[:],
-                in0=x_tile(i),
-                scalar1=column_of(rstds, i),
-                scalar2=shifts[i][:],
-                op0=ALU.mult,
-                op1=ALU.add,
+                out=centred[:].rearrange("p (c e q) -> p c e q", c=PACK, e=2),
+                in0=x_tile(i).rearrange("p (c q e) -> p c e q", c=PACK, e=2),
+                scalar1=column_of(neg_means, i),
+                scalar2=column_of(rstds, i),
+                op0=ALU.add,
+                op1=ALU.mult,
             )
             centreds[i] = centred
 
@@ -279,7 +251,14 @@ def tile_latentattentionblock_pa_t_kernel(tc, x, norm_w, expand_w, out_0, out_1,
                 turneds[i].append(turned)
 
         def apply_gain(i):
-            xn_grouped = work.tile([P, PASSES, P, PACK], BF16, align_bytes=64, name="xn_grouped")
+            xn_grouped = ring.tile(
+                [P, PASSES, P, PACK],
+                BF16,
+                name="xn_grouped",
+                tag="xn_grouped_%d" % (i % 3),
+                offset=(i % 3) * W * 4,
+                align_bytes=64,
+            )
             for g in range(PASSES):
                 gain = gain_t[:, g * PACK : (g + 1) * PACK].unsqueeze(1).to_broadcast([P, P, PACK])
                 nc.vector.tensor_tensor(
@@ -341,14 +320,23 @@ def tile_latentattentionblock_pa_t_kernel(tc, x, norm_w, expand_w, out_0, out_1,
             nc.vector.tensor_tensor(
                 out=geglu_stage[:, j, :], in0=hiddens[i][1][:, E - pre_in_0 : BANK], in1=gelus[i][:], op=ALU.mult
             )
-            if j == TILES_PER_GROUP - 1:
-                rows = slice(grp * GROUP_ROWS, (grp + 1) * GROUP_ROWS)
-                for dram, tile_ap in ((q_rows, qk_stage[:, 0, :, :]), (k_rows, qk_stage[:, 1, :, :]), (geglu_rows, geglu_stage[:])):
-                    nc.sync.dma_start(out=dram[rows, :].rearrange("(p j) c -> p j c", j=TILES_PER_GROUP), in_=tile_ap)
+            last = TILES_PER_GROUP - 1
+            if j == last:
+                store(grp, last if grp == GROUPS - 1 else 0, TILES_PER_GROUP)
+            elif grp == GROUPS - 1 and j == last - 1:
+                store(grp, 0, last)
+
+        def store(grp, j0, j1):
+            qk_stage, geglu_stage = stages[grp]
+            rows = slice(grp * GROUP_ROWS, (grp + 1) * GROUP_ROWS)
+            for dram, tile_ap in ((q_rows, qk_stage[:, 0, :, :]), (k_rows, qk_stage[:, 1, :, :]), (geglu_rows, geglu_stage[:])):
+                view = dram[rows, :].rearrange("(p j) c -> p j c", j=TILES_PER_GROUP)
+                nc.sync.dma_start(out=view[:, j0:j1, :], in_=tile_ap[:, j0:j1, :])
 
         def in_range(i):
             return 0 <= i < N_TILES
 
+        slots_of_step = {-1: (0, 1), 0: (2, 3, 4), 1: (5, 6, 7)}
         for step in range(FIRST_STEP, N_TILES + LAG_GATE):
             m, third = divmod(step + TRIPLE + RSTD_AHEAD - VECTOR_HEAD, TRIPLE)
             first = VECTOR_HEAD + m * TRIPLE
@@ -356,34 +344,42 @@ def tile_latentattentionblock_pa_t_kernel(tc, x, norm_w, expand_w, out_0, out_1,
             if in_range(step - LAG_QUANTISE):
                 quantise(step - LAG_QUANTISE)
             if in_range(step):
-                find_shift(step)
                 normalise(step)
+            if step == -1:
+                head_statistics(0)
+                vector_sum(0)
+                find_rstd(0)
+                head_statistics(1)
+            elif step == 0:
+                vector_sum(1)
+                head_statistics(2)
+                vector_sum(2)
+                find_rstd(1)
+            elif step == 1:
+                head_statistics(3)
             if third == 0 and m > 0 and first - TRIPLE < N_TILES:
-                vector_sum(first - TRIPLE + 1, TRIPLE)
+                vector_sum(first - TRIPLE + 1)
                 find_rstd(place[first - TRIPLE][0])
             if in_range(step - LAG_PROJECT):
                 project(step - LAG_PROJECT)
+            if step == 1:
+                turn_gain()
             if in_range(step - LAG_TURN):
                 turn(step - LAG_TURN)
-            if step + 1 < VECTOR_HEAD:
-                head_statistics(step + 1)
-            if step == 0:
-                turn_gain()
-            if step < 3:
-                slot = 2 * (step - FIRST_STEP)
-                turn_weights(slot, ())
-                turn_weights(slot + 1, (1,) if step < 2 else ())
+            for s in slots_of_step.get(step, ()):
+                turn_weights(s)
 
-            if in_range(step - LAG_GATE):
-                gate_vector(step - LAG_GATE)
-            if step + 1 < VECTOR_HEAD:
-                vector_sum(step + 1, 2)
-                find_rstd(place[step + 1][0])
             if in_range(step - LAG_GAIN):
                 apply_gain(step - LAG_GAIN)
+            if step == 2:
+                vector_sum(3)
+                head_statistics(4)
+                vector_sum(4)
+                find_rstd(2)
             if m >= 0 and first < N_TILES:
-                triple_vector(first, third)
-                triple_scalar(first, third)
+                triple_statistics(first, third)
+            if in_range(step - LAG_GATE):
+                gate_vector(step - LAG_GATE)
             if step in (2, 3):
                 quantise_weights(step - 2)
             if in_range(step - LAG_PROJECT):

@@ -37,7 +37,7 @@ LAG_GAIN = 2
 LAG_QUANTISE = 3
 LAG_PROJECT = 4
 LAG_GATE = 5
-RSTD_AHEAD = 1
+STATISTICS_AHEAD = 2
 FIRST_STEP = -1
 
 FLOPS = 2 * ROWS * W * N
@@ -135,7 +135,7 @@ def tile_latentattentionblock_pa_t_kernel(tc, x, norm_w, expand_w, out_0, out_1,
         for i in range(VECTOR_HEAD, N_TILES, TRIPLE):
             rstd_groups.append([i + 1, i, i + 2])
         place = {}
-        neg_means, sums, mean_vars, rstds, halves = {}, {}, {}, {}, {}
+        neg_means, sums, mean_vars, var_eps, rstds, halves = {}, {}, {}, {}, {}, {}
         for m, members in enumerate(rstd_groups):
             for column, i in enumerate(members):
                 place[i] = (m, column)
@@ -195,38 +195,41 @@ def tile_latentattentionblock_pa_t_kernel(tc, x, norm_w, expand_w, out_0, out_1,
                 vector_half(first + 1, half)
                 scalar_squares(first + 2 * half)
 
-        def find_rstd(m):
+        def head_sums(m):
             count = len(rstd_groups[m])
-            by_vector = 1 if count == TRIPLE else count
-            var_eps = small.tile([P, TRIPLE], F32, name="var_eps")
+            var_eps[m] = small.tile([P, TRIPLE], F32, name="var_eps")
             nc.gpsimd.tensor_scalar(
-                out=var_eps[:, 0:by_vector],
-                in0=mean_vars[m][:, 0:by_vector, 1],
+                out=var_eps[m][:, 0:count],
+                in0=mean_vars[m][:, 0:count, 1],
                 scalar1=float(W),
                 scalar2=W * EPS,
                 op0=ALU.mult,
                 op1=ALU.add,
             )
-            if by_vector < count:
-                nc.gpsimd.tensor_scalar(
-                    out=var_eps[:, by_vector:count],
-                    in0=sums[m][:, by_vector:count],
-                    scalar1=1.0,
-                    scalar2=W * EPS,
-                    op0=ALU.mult,
-                    op1=ALU.add,
-                )
             nc.gpsimd.tensor_scalar(
-                out=neg_means[m][:, 0:by_vector],
-                in0=mean_vars[m][:, 0:by_vector, 0],
+                out=neg_means[m][:, 0:count],
+                in0=mean_vars[m][:, 0:count, 0],
                 scalar1=-1.0,
                 scalar2=0.0,
                 op0=ALU.mult,
                 op1=ALU.add,
             )
+
+        def triple_join(m):
+            nc.scalar.activation(out=neg_means[m][:, 0:1], in_=mean_vars[m][:, 0, 0:1], func=ACT.Copy, scale=-1.0)
+            nc.scalar.activation(out=sums[m][:, 0:1], in_=mean_vars[m][:, 0, 1:2], func=ACT.Copy, scale=float(W))
+
+        def triple_sums(m):
+            var_eps[m] = small.tile([P, TRIPLE], F32, name="var_eps")
+            nc.gpsimd.tensor_scalar(
+                out=var_eps[m][:], in0=sums[m][:], scalar1=1.0, scalar2=W * EPS, op0=ALU.mult, op1=ALU.add
+            )
+
+        def find_rstd(m):
+            count = len(rstd_groups[m])
             rstds[m] = small.tile([P, TRIPLE], F32, name="rstd")
             nc.gpsimd.tensor_tensor(
-                out=rstds[m][:, 0:count], in0=var_eps[:, 0:count], in1=minus_half[:, 0:count], op=ALU.pow
+                out=rstds[m][:, 0:count], in0=var_eps[m][:, 0:count], in1=minus_half[:, 0:count], op=ALU.pow
             )
 
         def normalise(i):
@@ -259,7 +262,7 @@ def tile_latentattentionblock_pa_t_kernel(tc, x, norm_w, expand_w, out_0, out_1,
                 offset=(i % 3) * W * 4,
                 align_bytes=64,
             )
-            for g in range(PASSES):
+            for g in reversed(range(PASSES)):
                 gain = gain_t[:, g * PACK : (g + 1) * PACK].unsqueeze(1).to_broadcast([P, P, PACK])
                 nc.vector.tensor_tensor(
                     out=xn_grouped[:, g, :, :],
@@ -307,8 +310,8 @@ def tile_latentattentionblock_pa_t_kernel(tc, x, norm_w, expand_w, out_0, out_1,
                 stages[grp] = (qk_stage, geglu_stage)
             hidden_0, hidden_1 = hiddens[i]
             gelu = work.tile([P, E], F32, name="gelu")
-            nc.scalar.activation(out=gelu[:, 0:pre_in_0], in_=hidden_0[:, 2 * QK : BANK], func=ACT.Gelu)
             nc.scalar.activation(out=gelu[:, pre_in_0:E], in_=hidden_1[:, 0 : E - pre_in_0], func=ACT.Gelu)
+            nc.scalar.activation(out=gelu[:, 0:pre_in_0], in_=hidden_0[:, 2 * QK : BANK], func=ACT.Gelu)
             nc.scalar.copy(
                 out=stages[grp][0][:, :, j, :], in_=hidden_0[:, 0 : 2 * QK].rearrange("p (o c) -> p o c", o=2)
             )
@@ -338,8 +341,11 @@ def tile_latentattentionblock_pa_t_kernel(tc, x, norm_w, expand_w, out_0, out_1,
 
         slots_of_step = {-1: (0, 1), 0: (2, 3, 4), 1: (5, 6, 7)}
         for step in range(FIRST_STEP, N_TILES + LAG_GATE):
-            m, third = divmod(step + TRIPLE + RSTD_AHEAD - VECTOR_HEAD, TRIPLE)
-            first = VECTOR_HEAD + m * TRIPLE
+            under_way = []
+            for first in range(VECTOR_HEAD, N_TILES, TRIPLE):
+                start = first - TRIPLE - (1 if first == VECTOR_HEAD else STATISTICS_AHEAD)
+                if start <= step < first:
+                    under_way.append((first, step - start))
 
             if in_range(step - LAG_QUANTISE):
                 quantise(step - LAG_QUANTISE)
@@ -348,18 +354,23 @@ def tile_latentattentionblock_pa_t_kernel(tc, x, norm_w, expand_w, out_0, out_1,
             if step == -1:
                 head_statistics(0)
                 vector_sum(0)
+                head_sums(0)
                 find_rstd(0)
                 head_statistics(1)
             elif step == 0:
                 vector_sum(1)
                 head_statistics(2)
                 vector_sum(2)
+                head_sums(1)
                 find_rstd(1)
             elif step == 1:
                 head_statistics(3)
-            if third == 0 and m > 0 and first - TRIPLE < N_TILES:
-                vector_sum(first - TRIPLE + 1)
-                find_rstd(place[first - TRIPLE][0])
+            for first, turn_of in under_way:
+                if turn_of == TRIPLE:
+                    triple_join(place[first][0])
+                    triple_sums(place[first][0])
+                if step == first - 1:
+                    find_rstd(place[first][0])
             if in_range(step - LAG_PROJECT):
                 project(step - LAG_PROJECT)
             if step == 1:
@@ -375,11 +386,16 @@ def tile_latentattentionblock_pa_t_kernel(tc, x, norm_w, expand_w, out_0, out_1,
                 vector_sum(3)
                 head_statistics(4)
                 vector_sum(4)
+                head_sums(2)
                 find_rstd(2)
-            if m >= 0 and first < N_TILES:
-                triple_statistics(first, third)
+            for first, turn_of in under_way:
+                if turn_of < TRIPLE:
+                    triple_statistics(first, turn_of)
             if in_range(step - LAG_GATE):
                 gate_vector(step - LAG_GATE)
+            for first, turn_of in under_way:
+                if turn_of == TRIPLE - 1:
+                    vector_sum(first + 1)
             if step in (2, 3):
                 quantise_weights(step - 2)
             if in_range(step - LAG_PROJECT):

@@ -35,8 +35,8 @@ TRIPLE = 3
 LAG_TURN = 1
 LAG_GAIN = 2
 LAG_QUANTISE = 3
-LAG_PROJECT = 4
-LAG_GATE = 5
+LAG_PROJECT = 3
+LAG_GATE = 4
 STATISTICS_AHEAD = 2
 FIRST_STEP = -1
 
@@ -253,24 +253,23 @@ def tile_latentattentionblock_pa_t_kernel(tc, x, norm_w, expand_w, out_0, out_1,
                     nc.tensor.transpose(out=turned[:, t, :], in_=centreds[i][:, k0 : k0 + P], identity=ident_f32[:])
                 turneds[i].append(turned)
 
-        def apply_gain(i):
-            xn_grouped = ring.tile(
-                [P, PASSES, P, PACK],
-                BF16,
-                name="xn_grouped",
-                tag="xn_grouped_%d" % (i % 3),
-                offset=(i % 3) * W * 4,
-                align_bytes=64,
-            )
-            for g in reversed(range(PASSES)):
-                gain = gain_t[:, g * PACK : (g + 1) * PACK].unsqueeze(1).to_broadcast([P, P, PACK])
-                nc.vector.tensor_tensor(
-                    out=xn_grouped[:, g, :, :],
-                    in0=turneds[i][g][:].rearrange("p t r -> p r t"),
-                    in1=gain,
-                    op=ALU.mult,
+        def apply_gain(i, g):
+            if i not in xn_groupeds:
+                xn_groupeds[i] = ring.tile(
+                    [P, PASSES, P, PACK],
+                    BF16,
+                    name="xn_grouped",
+                    tag="xn_grouped_%d" % (i % 3),
+                    offset=(i % 3) * W * 4,
+                    align_bytes=64,
                 )
-            xn_groupeds[i] = xn_grouped
+            gain = gain_t[:, g * PACK : (g + 1) * PACK].unsqueeze(1).to_broadcast([P, P, PACK])
+            nc.vector.tensor_tensor(
+                out=xn_groupeds[i][:, g, :, :],
+                in0=turneds[i][g][:].rearrange("p t r -> p r t"),
+                in1=gain,
+                op=ALU.mult,
+            )
 
         def quantise(i):
             xn_codes = work.tile([P, PASSES, P], U32, align_bytes=64, name="xn_codes")
@@ -347,8 +346,13 @@ def tile_latentattentionblock_pa_t_kernel(tc, x, norm_w, expand_w, out_0, out_1,
                 if start <= step < first:
                     under_way.append((first, step - start))
 
+            behind_pow = step >= VECTOR_HEAD and (step - VECTOR_HEAD) % TRIPLE == 0
+            if behind_pow and in_range(step - LAG_GAIN):
+                apply_gain(step - LAG_GAIN, 1)
             if in_range(step - LAG_QUANTISE):
                 quantise(step - LAG_QUANTISE)
+            if step == 3:
+                quantise_weights(1)
             if in_range(step):
                 normalise(step)
             if step == -1:
@@ -365,23 +369,27 @@ def tile_latentattentionblock_pa_t_kernel(tc, x, norm_w, expand_w, out_0, out_1,
                 find_rstd(1)
             elif step == 1:
                 head_statistics(3)
-            for first, turn_of in under_way:
-                if turn_of == TRIPLE:
-                    triple_join(place[first][0])
-                    triple_sums(place[first][0])
-                if step == first - 1:
-                    find_rstd(place[first][0])
-            if in_range(step - LAG_PROJECT):
-                project(step - LAG_PROJECT)
             if step == 1:
                 turn_gain()
             if in_range(step - LAG_TURN):
                 turn(step - LAG_TURN)
             for s in slots_of_step.get(step, ()):
                 turn_weights(s)
+            if in_range(step - LAG_PROJECT):
+                project(step - LAG_PROJECT)
+            if in_range(step - LAG_GATE):
+                gate_scalar(step - LAG_GATE)
+            for first, turn_of in under_way:
+                if turn_of == TRIPLE:
+                    triple_join(place[first][0])
+                    triple_sums(place[first][0])
+                if step == first - 1:
+                    find_rstd(place[first][0])
 
             if in_range(step - LAG_GAIN):
-                apply_gain(step - LAG_GAIN)
+                if not behind_pow:
+                    apply_gain(step - LAG_GAIN, 1)
+                apply_gain(step - LAG_GAIN, 0)
             if step == 2:
                 vector_sum(3)
                 head_statistics(4)
@@ -396,7 +404,5 @@ def tile_latentattentionblock_pa_t_kernel(tc, x, norm_w, expand_w, out_0, out_1,
             for first, turn_of in under_way:
                 if turn_of == TRIPLE - 1:
                     vector_sum(first + 1)
-            if step in (2, 3):
-                quantise_weights(step - 2)
-            if in_range(step - LAG_PROJECT):
-                gate_scalar(step - LAG_PROJECT)
+            if step == 2:
+                quantise_weights(0)

@@ -37,7 +37,7 @@ LAG_GAIN = 2
 LAG_QUANTISE = 3
 LAG_PROJECT = 3
 LAG_GATE = 4
-STATISTICS_AHEAD = 2
+STATISTICS_AHEAD = 1
 FIRST_STEP = -1
 
 FLOPS = 2 * ROWS * W * N
@@ -65,10 +65,10 @@ def tile_latentattentionblock_pa_t_kernel(tc, x, norm_w, expand_w, out_0, out_1,
             x_group = resident.tile([P, TILES_PER_GROUP, W], BF16, name="x_group")
             x_groups.append(x_group)
 
-        def load_x(grp, j0, j1):
+        def load_x(grp, j0, j1, c0=0, c1=W):
             rows = x_rows[grp * GROUP_ROWS : (grp + 1) * GROUP_ROWS, :]
             view = rows.rearrange("(p j) k -> p j k", j=TILES_PER_GROUP)
-            nc.sync.dma_start(out=x_groups[grp][:, j0:j1, :], in_=view[:, j0:j1, :])
+            nc.sync.dma_start(out=x_groups[grp][:, j0:j1, c0:c1], in_=view[:, j0:j1, c0:c1])
 
         w_rows = const.tile([P, SLOTS, W], BF16)
 
@@ -76,13 +76,14 @@ def tile_latentattentionblock_pa_t_kernel(tc, x, norm_w, expand_w, out_0, out_1,
             rows = expand_w[row0 : row0 + (slot1 - slot0) * P, :]
             nc.sync.dma_start(out=w_rows[:, slot0:slot1, :], in_=rows.rearrange("(s p) k -> p s k", p=P))
 
-        load_x(0, 0, 1)
+        load_x(0, 0, 1, 0, W // 2)
+        load_x(0, 0, 1, W // 2, W)
         load_x(0, 1, 2)
         load_w(0, 2, 0)
         load_x(0, 2, 4)
         load_w(2, 5, 2 * QK + E)
-        load_w(5, 8, 2 * QK)
         load_x(1, 0, 1)
+        load_w(5, 8, 2 * QK)
         load_x(1, 1, TILES_PER_GROUP)
         for grp in range(2, GROUPS):
             load_x(grp, 0, TILES_PER_GROUP)
@@ -215,15 +216,14 @@ def tile_latentattentionblock_pa_t_kernel(tc, x, norm_w, expand_w, out_0, out_1,
                 op1=ALU.add,
             )
 
-        def triple_join(m):
-            nc.scalar.activation(out=neg_means[m][:, 0:1], in_=mean_vars[m][:, 0, 0:1], func=ACT.Copy, scale=-1.0)
-            nc.scalar.activation(out=sums[m][:, 0:1], in_=mean_vars[m][:, 0, 1:2], func=ACT.Copy, scale=float(W))
-
         def triple_sums(m):
             var_eps[m] = small.tile([P, TRIPLE], F32, name="var_eps")
-            nc.gpsimd.tensor_scalar(
-                out=var_eps[m][:], in0=sums[m][:], scalar1=1.0, scalar2=W * EPS, op0=ALU.mult, op1=ALU.add
-            )
+            for out, in_, scale, bias in (
+                (neg_means[m][:, 0:1], mean_vars[m][:, 0, 0:1], -1.0, 0.0),
+                (var_eps[m][:, 0:1], mean_vars[m][:, 0, 1:2], float(W), W * EPS),
+                (var_eps[m][:, 1:TRIPLE], sums[m][:, 1:TRIPLE], 1.0, W * EPS),
+            ):
+                nc.scalar.activation(out=out, in_=in_, func=ACT.Copy, scale=scale, bias=bias)
 
         def find_rstd(m):
             count = len(rstd_groups[m])
@@ -309,8 +309,12 @@ def tile_latentattentionblock_pa_t_kernel(tc, x, norm_w, expand_w, out_0, out_1,
                 stages[grp] = (qk_stage, geglu_stage)
             hidden_0, hidden_1 = hiddens[i]
             gelu = work.tile([P, E], F32, name="gelu")
-            nc.scalar.activation(out=gelu[:, pre_in_0:E], in_=hidden_1[:, 0 : E - pre_in_0], func=ACT.Gelu)
-            nc.scalar.activation(out=gelu[:, 0:pre_in_0], in_=hidden_0[:, 2 * QK : BANK], func=ACT.Gelu)
+            pieces = [
+                (gelu[:, pre_in_0:E], hidden_1[:, 0 : E - pre_in_0]),
+                (gelu[:, 0:pre_in_0], hidden_0[:, 2 * QK : BANK]),
+            ]
+            for out, in_ in reversed(pieces) if i == N_TILES - 1 else pieces:
+                nc.scalar.activation(out=out, in_=in_, func=ACT.Gelu)
             nc.scalar.copy(
                 out=stages[grp][0][:, :, j, :], in_=hidden_0[:, 0 : 2 * QK].rearrange("p (o c) -> p o c", o=2)
             )
@@ -342,14 +346,14 @@ def tile_latentattentionblock_pa_t_kernel(tc, x, norm_w, expand_w, out_0, out_1,
         for step in range(FIRST_STEP, N_TILES + LAG_GATE):
             under_way = []
             for first in range(VECTOR_HEAD, N_TILES, TRIPLE):
-                start = first - TRIPLE - (1 if first == VECTOR_HEAD else STATISTICS_AHEAD)
+                start = first - TRIPLE - STATISTICS_AHEAD
                 if start <= step < first:
                     under_way.append((first, step - start))
 
             behind_pow = step >= VECTOR_HEAD and (step - VECTOR_HEAD) % TRIPLE == 0
             if behind_pow and in_range(step - LAG_GAIN):
                 apply_gain(step - LAG_GAIN, 1)
-            if in_range(step - LAG_QUANTISE):
+            if 0 <= step - LAG_QUANTISE < N_TILES - 1:
                 quantise(step - LAG_QUANTISE)
             if step == 3:
                 quantise_weights(1)
@@ -369,10 +373,16 @@ def tile_latentattentionblock_pa_t_kernel(tc, x, norm_w, expand_w, out_0, out_1,
                 find_rstd(1)
             elif step == 1:
                 head_statistics(3)
-            if step == 1:
-                turn_gain()
+                vector_sum(3)
+                head_statistics(4)
+                vector_sum(4)
+            elif step == 2:
+                head_sums(2)
+                find_rstd(2)
             if in_range(step - LAG_TURN):
                 turn(step - LAG_TURN)
+            if step == 1:
+                turn_gain()
             for s in slots_of_step.get(step, ()):
                 turn_weights(s)
             if in_range(step - LAG_PROJECT):
@@ -381,7 +391,6 @@ def tile_latentattentionblock_pa_t_kernel(tc, x, norm_w, expand_w, out_0, out_1,
                 gate_scalar(step - LAG_GATE)
             for first, turn_of in under_way:
                 if turn_of == TRIPLE:
-                    triple_join(place[first][0])
                     triple_sums(place[first][0])
                 if step == first - 1:
                     find_rstd(place[first][0])
@@ -390,12 +399,8 @@ def tile_latentattentionblock_pa_t_kernel(tc, x, norm_w, expand_w, out_0, out_1,
                 if not behind_pow:
                     apply_gain(step - LAG_GAIN, 1)
                 apply_gain(step - LAG_GAIN, 0)
-            if step == 2:
-                vector_sum(3)
-                head_statistics(4)
-                vector_sum(4)
-                head_sums(2)
-                find_rstd(2)
+            if step - LAG_GAIN == N_TILES - 1:
+                quantise(N_TILES - 1)
             for first, turn_of in under_way:
                 if turn_of < TRIPLE:
                     triple_statistics(first, turn_of)

@@ -30,6 +30,7 @@ GROUP_ROWS = TILES_PER_GROUP * P
 GROUPS = ROWS // GROUP_ROWS
 N_TILES = ROWS // P
 VECTOR_HEAD = 5
+SCALAR_HEAD = 1
 TRIPLE = 3
 
 LAG_TURN = 1
@@ -79,11 +80,13 @@ def tile_latentattentionblock_pa_t_kernel(tc, x, norm_w, expand_w, out_0, out_1,
         load_x(0, 0, 1, 0, W // 2)
         load_x(0, 0, 1, W // 2, W)
         load_x(0, 1, 2)
-        load_w(0, 2, 0)
         load_x(0, 2, 4)
-        load_w(2, 5, 2 * QK + E)
+        load_w(0, 1, 0)
+        load_w(1, 2, 2 * QK + E)
+        load_w(2, 4, 2 * QK + E + P)
         load_x(1, 0, 1)
-        load_w(5, 8, 2 * QK)
+        load_w(4, 6, QK)
+        load_w(6, 8, QK + 2 * P)
         load_x(1, 1, TILES_PER_GROUP)
         for grp in range(2, GROUPS):
             load_x(grp, 0, TILES_PER_GROUP)
@@ -119,9 +122,10 @@ def tile_latentattentionblock_pa_t_kernel(tc, x, norm_w, expand_w, out_0, out_1,
             words = w_rows[:, s, :].bitcast(F32)
             for c in range(PACK):
                 nc.tensor.transpose(out=w_turned[:, c, :], in_=words[:, c * P : (c + 1) * P], identity=ident_f32[:])
-            dst = w_grouped[:, :, s * P : (s + 1) * P, :].bitcast(F32)
-            src = w_turned[:].rearrange("p (g u) n -> p g n u", g=PASSES)
-            nc.scalar.copy(out=dst, in_=src)
+            for g in range(PASSES):
+                dst = w_grouped[:, g, s * P : (s + 1) * P, :].bitcast(F32)
+                src = w_turned[:, 2 * g : 2 * g + 2, :].rearrange("p u n -> p n u")
+                nc.scalar.copy(out=dst, in_=src)
 
         def quantise_weights(bank):
             cols = slice(bank * BANK, (bank + 1) * BANK)
@@ -132,7 +136,7 @@ def tile_latentattentionblock_pa_t_kernel(tc, x, norm_w, expand_w, out_0, out_1,
                     in_=w_grouped[:, g, cols, :].rearrange("p n t -> p (n t)"),
                 )
 
-        rstd_groups = [[0], [1, 2], [3, 4]]
+        rstd_groups = [[0], [2, SCALAR_HEAD], [3, 4]]
         for i in range(VECTOR_HEAD, N_TILES, TRIPLE):
             rstd_groups.append([i + 1, i, i + 2])
         place = {}
@@ -198,23 +202,14 @@ def tile_latentattentionblock_pa_t_kernel(tc, x, norm_w, expand_w, out_0, out_1,
 
         def head_sums(m):
             count = len(rstd_groups[m])
+            by_vector = count - (SCALAR_HEAD in rstd_groups[m])
             var_eps[m] = small.tile([P, TRIPLE], F32, name="var_eps")
-            nc.gpsimd.tensor_scalar(
-                out=var_eps[m][:, 0:count],
-                in0=mean_vars[m][:, 0:count, 1],
-                scalar1=float(W),
-                scalar2=W * EPS,
-                op0=ALU.mult,
-                op1=ALU.add,
-            )
-            nc.gpsimd.tensor_scalar(
-                out=neg_means[m][:, 0:count],
-                in0=mean_vars[m][:, 0:count, 0],
-                scalar1=-1.0,
-                scalar2=0.0,
-                op0=ALU.mult,
-                op1=ALU.add,
-            )
+            for out, in_, scale, bias in (
+                (var_eps[m][:, 0:by_vector], mean_vars[m][:, 0:by_vector, 1], float(W), W * EPS),
+                (var_eps[m][:, by_vector:count], sums[m][:, by_vector:count], 1.0, W * EPS),
+                (neg_means[m][:, 0:by_vector], mean_vars[m][:, 0:by_vector, 0], -1.0, 0.0),
+            )[:: 1 if by_vector < count else 2]:
+                nc.gpsimd.tensor_scalar(out=out, in0=in_, scalar1=scale, scalar2=bias, op0=ALU.mult, op1=ALU.add)
 
         def triple_sums(m):
             var_eps[m] = small.tile([P, TRIPLE], F32, name="var_eps")
@@ -299,32 +294,27 @@ def tile_latentattentionblock_pa_t_kernel(tc, x, norm_w, expand_w, out_0, out_1,
                     )
                 hiddens[i].append(hidden)
 
-        pre_in_0 = BANK - 2 * QK
-
         def gate_scalar(i):
             grp, j = divmod(i, TILES_PER_GROUP)
             if j == 0:
                 qk_stage = stage.tile([P, 2, TILES_PER_GROUP, QK], F32, name="qk_stage")
                 geglu_stage = stage.tile([P, TILES_PER_GROUP, E], F32, name="geglu_stage")
                 stages[grp] = (qk_stage, geglu_stage)
+            qk_stage = stages[grp][0]
             hidden_0, hidden_1 = hiddens[i]
-            gelu = work.tile([P, E], F32, name="gelu")
-            pieces = [
-                (gelu[:, pre_in_0:E], hidden_1[:, 0 : E - pre_in_0]),
-                (gelu[:, 0:pre_in_0], hidden_0[:, 2 * QK : BANK]),
-            ]
-            for out, in_ in reversed(pieces) if i == N_TILES - 1 else pieces:
-                nc.scalar.activation(out=out, in_=in_, func=ACT.Gelu)
-            nc.scalar.copy(
-                out=stages[grp][0][:, :, j, :], in_=hidden_0[:, 0 : 2 * QK].rearrange("p (o c) -> p o c", o=2)
-            )
-            gelus[i] = gelu
+            gelus[i] = work.tile([P, E], F32, name="gelu")
+            if i < N_TILES - 1:
+                nc.scalar.copy(out=qk_stage[:, 1, j, :], in_=hidden_1[:, 0:QK])
+            nc.scalar.activation(out=gelus[i][:], in_=hidden_0[:, QK:BANK], func=ACT.Gelu)
+            if i == N_TILES - 1:
+                nc.scalar.copy(out=qk_stage[:, 1, j, :], in_=hidden_1[:, 0:QK])
+            nc.scalar.copy(out=qk_stage[:, 0, j, :], in_=hidden_0[:, 0:QK])
 
         def gate_vector(i):
             grp, j = divmod(i, TILES_PER_GROUP)
-            qk_stage, geglu_stage = stages[grp]
+            geglu_stage = stages[grp][1]
             nc.vector.tensor_tensor(
-                out=geglu_stage[:, j, :], in0=hiddens[i][1][:, E - pre_in_0 : BANK], in1=gelus[i][:], op=ALU.mult
+                out=geglu_stage[:, j, :], in0=hiddens[i][1][:, QK:BANK], in1=gelus[i][:], op=ALU.mult
             )
             last = TILES_PER_GROUP - 1
             if j == last:
@@ -342,7 +332,7 @@ def tile_latentattentionblock_pa_t_kernel(tc, x, norm_w, expand_w, out_0, out_1,
         def in_range(i):
             return 0 <= i < N_TILES
 
-        slots_of_step = {-1: (0, 1), 0: (2, 3, 4), 1: (5, 6, 7)}
+        slots_of_step = {-1: (0, 1), 0: (2, 3), 1: (4, 5, 6, 7)}
         for step in range(FIRST_STEP, N_TILES + LAG_GATE):
             under_way = []
             for first in range(VECTOR_HEAD, N_TILES, TRIPLE):
@@ -364,15 +354,15 @@ def tile_latentattentionblock_pa_t_kernel(tc, x, norm_w, expand_w, out_0, out_1,
                 vector_sum(0)
                 head_sums(0)
                 find_rstd(0)
-                head_statistics(1)
-            elif step == 0:
-                vector_sum(1)
                 head_statistics(2)
+                scalar_mean(SCALAR_HEAD)
+                scalar_squares(SCALAR_HEAD)
+            elif step == 0:
                 vector_sum(2)
                 head_sums(1)
                 find_rstd(1)
-            elif step == 1:
                 head_statistics(3)
+            elif step == 1:
                 vector_sum(3)
                 head_statistics(4)
                 vector_sum(4)
@@ -395,6 +385,8 @@ def tile_latentattentionblock_pa_t_kernel(tc, x, norm_w, expand_w, out_0, out_1,
                 if step == first - 1:
                     find_rstd(place[first][0])
 
+            if step == 1:
+                quantise_weights(0)
             if in_range(step - LAG_GAIN):
                 if not behind_pow:
                     apply_gain(step - LAG_GAIN, 1)
@@ -409,5 +401,3 @@ def tile_latentattentionblock_pa_t_kernel(tc, x, norm_w, expand_w, out_0, out_1,
             for first, turn_of in under_way:
                 if turn_of == TRIPLE - 1:
                     vector_sum(first + 1)
-            if step == 2:
-                quantise_weights(0)

from contextlib import ExitStack

import concourse.mybir as mybir
from concourse.masks import make_identity

F32 = mybir.dt.float32
BF16 = mybir.dt.bfloat16
U32 = mybir.dt.uint32
U8 = mybir.dt.uint8
FP8X4 = mybir.dt.float8_e4m3fn_x4
ACT = mybir.ActivationFunctionType
ALU = mybir.AluOpType

P = 128
PACK = 4
K_PASS = P * PACK
BANK = 512

ROWS = 4 * 1024
W = 1024
QK = 128
E = 384
N = 2 * QK + 2 * E
EPS = 1e-5

PASSES = W // K_PASS
SLOTS = N // P
TILES_PER_GROUP = 4
GROUP_ROWS = TILES_PER_GROUP * P
GROUPS = ROWS // GROUP_ROWS
N_TILES = ROWS // P
VECTOR_HEAD = 5
SCALAR_HEAD = 1
TRIPLE = 3

LAG_TURN = 1
LAG_GAIN = 2
LAG_QUANTISE = 3
LAG_PROJECT = 3
LAG_GATE = 4
STATISTICS_AHEAD = 1
FIRST_STEP = -1

FLOPS = 2 * ROWS * W * N


def tile_latentattentionblock_pa_t_kernel(tc, x, norm_w, expand_w, out_0, out_1, out_2):
    nc = tc.nc
    x_rows = x.flatten_outer_dims()
    q_rows = out_0.flatten_outer_dims()
    k_rows = out_1.flatten_outer_dims()
    geglu_rows = out_2.flatten_outer_dims()

    with ExitStack() as pools:
        pools.enter_context(tc.manual_schedule())
        const = pools.enter_context(tc.tile_pool(name="const", bufs=1))
        resident = pools.enter_context(tc.tile_pool(name="resident", bufs=GROUPS))
        small = pools.enter_context(tc.tile_pool(name="small", bufs=4))
        work = pools.enter_context(tc.tile_pool(name="work", bufs=3))
        stage = pools.enter_context(tc.tile_pool(name="stage", bufs=2))
        ring = pools.enter_context(tc.tile_pool(name="ring", bufs=1))
        psum = pools.enter_context(tc.psum_pool(name="psum", bufs=4))

        x_groups = []
        for grp in range(GROUPS):
            x_group = resident.tile([P, TILES_PER_GROUP, W], BF16, name="x_group")
            x_groups.append(x_group)

        def load_x(grp, j0, j1, c0=0, c1=W):
            rows = x_rows[grp * GROUP_ROWS : (grp + 1) * GROUP_ROWS, :]
            view = rows.rearrange("(p j) k -> p j k", j=TILES_PER_GROUP)
            nc.sync.dma_start(out=x_groups[grp][:, j0:j1, c0:c1], in_=view[:, j0:j1, c0:c1])

        w_rows = const.tile([P, SLOTS, W], BF16)

        def load_w(slot0, slot1, row0):
            rows = expand_w[row0 : row0 + (slot1 - slot0) * P, :]
            nc.sync.dma_start(out=w_rows[:, slot0:slot1, :], in_=rows.rearrange("(s p) k -> p s k", p=P))

        load_x(0, 0, 1, 0, W // 2)
        load_x(0, 0, 1, W // 2, W)
        load_x(0, 1, 2)
        load_x(0, 2, 4)
        load_w(0, 1, 0)
        load_w(1, 2, 2 * QK + E)
        load_w(2, 4, 2 * QK + E + P)
        load_x(1, 0, 1)
        load_w(4, 6, QK)
        load_w(6, 8, QK + 2 * P)
        load_x(1, 1, TILES_PER_GROUP)
        for grp in range(2, GROUPS):
            load_x(grp, 0, TILES_PER_GROUP)

        ident_f32 = const.tile([P, P], F32)
        make_identity(nc, ident_f32[:])
        minus_half = const.tile([P, TRIPLE], F32)
        nc.vector.memset(minus_half[:], -0.5)

        table_in = const.tile([P, 1], F32)
        nc.vector.memset(table_in[:], 0.0)
        table_out = const.tile([P, 1], F32)
        nc.scalar.activation(out=table_out[:], in_=table_in[:], func=ACT.Gelu)

        gain_rows = const.tile([P, 2 * P], BF16)
        nc.vector.memset(gain_rows[:], 0.0)
        nc.scalar.dma_start(out=gain_rows[0 : W // (2 * P), :], in_=norm_w.rearrange("(c k) -> c k", k=2 * P))
        gain_t = const.tile([P, W // P], F32)

        def turn_gain():
            gain_ps = psum.tile([P, P], F32, tag="turned")
            nc.tensor.transpose(out=gain_ps[:], in_=gain_rows[:].bitcast(F32), identity=ident_f32[:])
            nc.vector.tensor_scalar(
                out=gain_t[:], in0=gain_ps[:].bitcast(BF16)[:, 0 : W // P], scalar1=32.0, scalar2=None, op0=ALU.mult
            )

        w_grouped = const.tile([P, PASSES, N, PACK], BF16, align_bytes=64)
        w_codes = const.tile([P, PASSES, N], U32, align_bytes=64)
        w_scales = const.tile([P, PASSES, N], U8, align_bytes=64)

        def turn_weights(s):
            w_turned = psum.tile([P, PACK, P], F32, tag="hidden", name="w_turned")
            words = w_rows[:, s, :].bitcast(F32)
            for c in range(PACK):
                nc.tensor.transpose(out=w_turned[:, c, :], in_=words[:, c * P : (c + 1) * P], identity=ident_f32[:])
            for g in range(PASSES):
                dst = w_grouped[:, g, s * P : (s + 1) * P, :].bitcast(F32)
                src = w_turned[:, 2 * g : 2 * g + 2, :].rearrange("p u n -> p n u")
                nc.scalar.copy(out=dst, in_=src)

        def quantise_weights(bank):
            cols = slice(bank * BANK, (bank + 1) * BANK)
            for g in range(PASSES):
                nc.vector.quantize_mx(
                    out=w_codes[:, g, cols].bitcast(FP8X4),
                    scales=w_scales[:, g, cols],
                    in_=w_grouped[:, g, cols, :].rearrange("p n t -> p (n t)"),
                )

        rstd_groups = [[0], [2, SCALAR_HEAD], [3, 4]]
        for i in range(VECTOR_HEAD, N_TILES, TRIPLE):
            rstd_groups.append([i + 1, i, i + 2])
        place = {}
        neg_means, sums, mean_vars, var_eps, rstds, halves = {}, {}, {}, {}, {}, {}
        for m, members in enumerate(rstd_groups):
            for column, i in enumerate(members):
                place[i] = (m, column)
        centreds, turneds, xn_groupeds = {}, {}, {}
        xn_codess, xn_scaless, hiddens, gelus, stages = {}, {}, {}, {}, {}

        def x_tile(i):
            return x_groups[i // TILES_PER_GROUP][:, i % TILES_PER_GROUP, :]

        def column_of(tiles, i):
            m, column = place[i]
            return tiles[m][:, column : column + 1]

        def open_group(m):
            neg_means[m] = small.tile([P, TRIPLE], F32, name="neg_means")
            sums[m] = small.tile([P, TRIPLE], F32, name="sums")
            mean_vars[m] = small.tile([P, 2, 2], F32, name="mean_vars")

        def vector_half(i, half):
            if half == 0:
                halves[i] = small.tile([P, 2, 6], F32, name="halves")
            nc.vector.bn_stats(out=halves[i][:, half, :], in_=x_tile(i)[:, half * 512 : (half + 1) * 512])

        def vector_sum(i):
            m, column = place[i]
            nc.vector.bn_aggr(out=mean_vars[m][:, column, :], in_=halves[i][:].rearrange("p h s -> p (h s)"))

        def scalar_mean(i):
            unread_a = work.tile([P, W], BF16, name="unread_a")
            nc.scalar.activation(
                out=unread_a[:], in_=x_tile(i), func=ACT.Copy, scale=-1.0 / W, accum_out=column_of(neg_means, i)
            )

        def scalar_squares(i):
            unread_b = work.tile([P, W], BF16, name="unread_b")
            nc.scalar.activation(
                out=unread_b[:],
                in_=x_tile(i),
                func=ACT.Square,
                bias=column_of(neg_means, i),
                accum_out=column_of(sums, i),
            )

        def head_statistics(i):
            if place[i][1] == 0:
                open_group(place[i][0])
            vector_half(i, 0)
            vector_half(i, 1)

        def triple_statistics(first, third):
            if third == 0:
                open_group(place[first][0])
                scalar_mean(first)
                scalar_mean(first + 2)
            else:
                half = third - 1
                vector_half(first + 1, half)
                scalar_squares(first + 2 * half)

        def head_sums(m):
            count = len(rstd_groups[m])
            by_vector = count - (SCALAR_HEAD in rstd_groups[m])
            var_eps[m] = small.tile([P, TRIPLE], F32, name="var_eps")
            for out, in_, scale, bias in (
                (var_eps[m][:, 0:by_vector], mean_vars[m][:, 0:by_vector, 1], float(W), W * EPS),
                (var_eps[m][:, by_vector:count], sums[m][:, by_vector:count], 1.0, W * EPS),
                (neg_means[m][:, 0:by_vector], mean_vars[m][:, 0:by_vector, 0], -1.0, 0.0),
            )[:: 1 if by_vector < count else 2]:
                nc.gpsimd.tensor_scalar(out=out, in0=in_, scalar1=scale, scalar2=bias, op0=ALU.mult, op1=ALU.add)

        def triple_sums(m):
            var_eps[m] = small.tile([P, TRIPLE], F32, name="var_eps")
            for out, in_, scale, bias in (
                (neg_means[m][:, 0:1], mean_vars[m][:, 0, 0:1], -1.0, 0.0),
                (var_eps[m][:, 0:1], mean_vars[m][:, 0, 1:2], float(W), W * EPS),
                (var_eps[m][:, 1:TRIPLE], sums[m][:, 1:TRIPLE], 1.0, W * EPS),
            ):
                nc.scalar.activation(out=out, in_=in_, func=ACT.Copy, scale=scale, bias=bias)

        def find_rstd(m):
            count = len(rstd_groups[m])
            rstds[m] = small.tile([P, TRIPLE], F32, name="rstd")
            nc.gpsimd.tensor_tensor(
                out=rstds[m][:, 0:count], in0=var_eps[m][:, 0:count], in1=minus_half[:, 0:count], op=ALU.pow
            )

        def normalise(i):
            centred = ring.tile([P, W], F32, name="centred", tag="centred_%d" % (i % 3), offset=(i % 3) * W * 4, align_bytes=64)
            nc.gpsimd.tensor_scalar(
                out=centred[:].rearrange("p (c e q) -> p c e q", c=PACK, e=2),
                in0=x_tile(i).rearrange("p (c q e) -> p c e q", c=PACK, e=2),
                scalar1=column_of(neg_means, i),
                scalar2=column_of(rstds, i),
                op0=ALU.add,
                op1=ALU.mult,
            )
            centreds[i] = centred

        def turn(i):
            turneds[i] = []
            for g in range(PASSES):
                turned = psum.tile([P, PACK, P], F32, tag="turned", name="turned")
                for t in range(PACK):
                    k0 = g * K_PASS + t * P
                    nc.tensor.transpose(out=turned[:, t, :], in_=centreds[i][:, k0 : k0 + P], identity=ident_f32[:])
                turneds[i].append(turned)

        def apply_gain(i, g):
            if i not in xn_groupeds:
                xn_groupeds[i] = ring.tile(
                    [P, PASSES, P, PACK],
                    BF16,
                    name="xn_grouped",
                    tag="xn_grouped_%d" % (i % 3),
                    offset=(i % 3) * W * 4,
                    align_bytes=64,
                )
            gain = gain_t[:, g * PACK : (g + 1) * PACK].unsqueeze(1).to_broadcast([P, P, PACK])
            nc.vector.tensor_tensor(
                out=xn_groupeds[i][:, g, :, :],
                in0=turneds[i][g][:].rearrange("p t r -> p r t"),
                in1=gain,
                op=ALU.mult,
            )

        def quantise(i):
            xn_codes = work.tile([P, PASSES, P], U32, align_bytes=64, name="xn_codes")
            xn_scales = work.tile([P, PASSES, P], U8, align_bytes=64, name="xn_scales")
            nc.vector.quantize_mx(
                out=xn_codes[:].rearrange("p g r -> p (g r)").bitcast(FP8X4),
                scales=xn_scales[:].rearrange("p g r -> p (g r)"),
                in_=xn_groupeds[i][:].rearrange("p g r t -> p (g r t)"),
            )
            xn_codess[i] = xn_codes
            xn_scaless[i] = xn_scales

        def project(i):
            hiddens[i] = []
            for bank in range(N // BANK):
                cols = slice(bank * BANK, (bank + 1) * BANK)
                hidden = psum.tile([P, BANK], F32, tag="hidden", name="hidden")
                for g in range(PASSES):
                    nc.tensor.matmul_mx(
                        out=hidden[:],
                        lhsT=xn_codess[i][:, g, :].bitcast(FP8X4),
                        lhsT_scale=xn_scaless[i][:, g, :],
                        rhs=w_codes[:, g, cols].bitcast(FP8X4),
                        rhs_scale=w_scales[:, g, cols],
                        start=(g == 0),
                        stop=(g == PASSES - 1),
                    )
                hiddens[i].append(hidden)

        def gate_scalar(i):
            grp, j = divmod(i, TILES_PER_GROUP)
            if j == 0:
                qk_stage = stage.tile([P, 2, TILES_PER_GROUP, QK], F32, name="qk_stage")
                geglu_stage = stage.tile([P, TILES_PER_GROUP, E], F32, name="geglu_stage")
                stages[grp] = (qk_stage, geglu_stage)
            qk_stage = stages[grp][0]
            hidden_0, hidden_1 = hiddens[i]
            gelus[i] = work.tile([P, E], F32, name="gelu")
            if i < N_TILES - 1:
                nc.scalar.copy(out=qk_stage[:, 1, j, :], in_=hidden_1[:, 0:QK])
            nc.scalar.activation(out=gelus[i][:], in_=hidden_0[:, QK:BANK], func=ACT.Gelu)
            if i == N_TILES - 1:
                nc.scalar.copy(out=qk_stage[:, 1, j, :], in_=hidden_1[:, 0:QK])
            nc.scalar.copy(out=qk_stage[:, 0, j, :], in_=hidden_0[:, 0:QK])

        def gate_vector(i):
            grp, j = divmod(i, TILES_PER_GROUP)
            geglu_stage = stages[grp][1]
            nc.vector.tensor_tensor(
                out=geglu_stage[:, j, :], in0=hiddens[i][1][:, QK:BANK], in1=gelus[i][:], op=ALU.mult
            )
            last = TILES_PER_GROUP - 1
            if j == last:
                store(grp, last if grp == GROUPS - 1 else 0, TILES_PER_GROUP)
            elif grp == GROUPS - 1 and j == last - 1:
                store(grp, 0, last)

        def store(grp, j0, j1):
            qk_stage, geglu_stage = stages[grp]
            rows = slice(grp * GROUP_ROWS, (grp + 1) * GROUP_ROWS)
            for dram, tile_ap in ((q_rows, qk_stage[:, 0, :, :]), (k_rows, qk_stage[:, 1, :, :]), (geglu_rows, geglu_stage[:])):
                view = dram[rows, :].rearrange("(p j) c -> p j c", j=TILES_PER_GROUP)
                nc.sync.dma_start(out=view[:, j0:j1, :], in_=tile_ap[:, j0:j1, :])

        def in_range(i):
            return 0 <= i < N_TILES

        slots_of_step = {-1: (0, 1), 0: (2, 3), 1: (4, 5, 6, 7)}
        for step in range(FIRST_STEP, N_TILES + LAG_GATE):
            under_way = []
            for first in range(VECTOR_HEAD, N_TILES, TRIPLE):
                start = first - TRIPLE - STATISTICS_AHEAD
                if start <= step < first:
                    under_way.append((first, step - start))

            behind_pow = step >= VECTOR_HEAD and (step - VECTOR_HEAD) % TRIPLE == 0
            if behind_pow and in_range(step - LAG_GAIN):
                apply_gain(step - LAG_GAIN, 1)
            if 0 <= step - LAG_QUANTISE < N_TILES - 1:
                quantise(step - LAG_QUANTISE)
            if step == 3:
                quantise_weights(1)
            if in_range(step):
                normalise(step)
            if step == -1:
                head_statistics(0)
                vector_sum(0)
                head_sums(0)
                find_rstd(0)
                head_statistics(2)
                scalar_mean(SCALAR_HEAD)
                scalar_squares(SCALAR_HEAD)
            elif step == 0:
                vector_sum(2)
                head_sums(1)
                find_rstd(1)
                head_statistics(3)
            elif step == 1:
                vector_sum(3)
                head_statistics(4)
                vector_sum(4)
            elif step == 2:
                head_sums(2)
                find_rstd(2)
            if in_range(step - LAG_TURN):
                turn(step - LAG_TURN)
            if step == 1:
                turn_gain()
            for s in slots_of_step.get(step, ()):
                turn_weights(s)
            if in_range(step - LAG_PROJECT):
                project(step - LAG_PROJECT)
            if in_range(step - LAG_GATE):
                gate_scalar(step - LAG_GATE)
            for first, turn_of in under_way:
                if turn_of == TRIPLE:
                    triple_sums(place[first][0])
                if step == first - 1:
                    find_rstd(place[first][0])

            if step == 1:
                quantise_weights(0)
            if in_range(step - LAG_GAIN):
                if not behind_pow:
                    apply_gain(step - LAG_GAIN, 1)
                apply_gain(step - LAG_GAIN, 0)
            if step - LAG_GAIN == N_TILES - 1:
                quantise(N_TILES - 1)
            for first, turn_of in under_way:
                if turn_of < TRIPLE:
                    triple_statistics(first, turn_of)
            if in_range(step - LAG_GATE):
                gate_vector(step - LAG_GATE)
            for first, turn_of in under_way:
                if turn_of == TRIPLE - 1:
                    vector_sum(first + 1)
